import numpy as np
import ml_dtypes


def mxq(x, axis, fmt="e4m3"):
    dtype, down = {"e4m3": (ml_dtypes.float8_e4m3fn, 7), "e5m2": (ml_dtypes.float8_e5m2, 14)}[fmt]
    v = np.moveaxis(np.asarray(x, np.float32).astype(ml_dtypes.bfloat16).astype(np.float64), axis, -1)
    blocks = v.reshape(v.shape[:-1] + (-1, 32))
    amax = np.abs(blocks).max(-1, keepdims=True)
    byte = np.maximum(np.where(amax > 0, np.frexp(amax)[1] - 1 + 127, 0) - down, 1)
    scale = np.exp2(byte - 127.0)
    codes = (blocks / scale).astype(np.float32).astype(dtype).astype(np.float64)
    return np.moveaxis((codes * scale).reshape(v.shape), -1, axis)


WIDE = False


def mx_kscale(k):
    if not WIDE:
        return np.ones(k)
    levels = np.array([10, -10, 5, -5, 0])
    a = np.random.permutation(np.resize(levels, k // 512 * 4)).reshape(k // 512, 4)
    idx = np.arange(k)
    return np.exp2(a[idx // 512, idx % 128 // 32])


BF16 = ml_dtypes.bfloat16


def bf(x):
    return np.asarray(x, np.float32).astype(BF16)


def f64(x):
    return np.asarray(x).astype(np.float64)


E2M1 = np.array([0.0, 0.5, 1.0, 1.5, 2.0, 3.0, 4.0, 6.0, -0.0, -0.5, -1.0, -1.5, -2.0, -3.0, -4.0, -6.0])


def pack_weight(w, fmt):
    k, n = w.shape
    w = f64(bf(w)).reshape(k // 32, 32, n)
    amax = np.abs(w).max(1)
    if fmt == "e4m3":
        byte = np.frexp(amax)[1] - 1 + 127 - 7
    else:
        mant, ex = np.frexp(amax / 6.0)
        byte = np.where(mant > 0.5, ex, ex - 1) + 127
    byte = np.clip(np.where(amax > 0, byte, 1), 1, 254)
    scaled = (w * np.exp2(127.0 - byte)[:, None, :]).reshape(k, n).astype(np.float32)
    by_word = np.ascontiguousarray(scaled.reshape(k // 512, 128, 4, n).transpose(0, 1, 3, 2))
    if fmt == "e4m3":
        words = by_word.astype(ml_dtypes.float8_e4m3fn).view(np.uint8)
    else:
        c = by_word.astype(ml_dtypes.float4_e2m1fn).view(np.uint8) & 0xF
        words = c[..., 0::2] | (c[..., 1::2] << 4)
    return np.ascontiguousarray(words), np.ascontiguousarray(byte.astype(np.uint8).reshape(k // 512, 16, n))


def unpack_weight(words, scales, fmt):
    g, p, n, _ = words.shape
    if fmt == "e4m3":
        vals = np.ascontiguousarray(words).view(ml_dtypes.float8_e4m3fn).astype(np.float64)
    else:
        nib = np.empty((g, p, n, 4), np.uint8)
        nib[..., 0::2] = words & 0xF
        nib[..., 1::2] = words >> 4
        vals = E2M1[nib]
    vals = vals * np.repeat(np.exp2(scales.astype(np.float64) - 127.0), 8, axis=1)[..., None]
    return vals.transpose(0, 1, 3, 2).reshape(g * 512, n)


B, IN_DIM, MEM = 512, 16128, 256
DIN = MEM + IN_DIM
F = 2 * MEM
LN_EPS = 1e-5
FMT = "e4m3"


def erf(v):
    a = np.minimum(np.abs(v), 6.0)
    a2 = 2.0 * a * a
    term = a.copy()
    tot = a.copy()
    for n in range(1, 120):
        term = term * a2 / (2 * n + 1)
        tot = tot + term
    return np.sign(v) * (2.0 / np.sqrt(np.pi)) * np.exp(-a * a) * tot


def gelu_erf(v):
    return 0.5 * v * (1.0 + erf(v / np.sqrt(2.0)))


def layernorm(t, g, b):
    mu = t.mean(-1, keepdims=True)
    var = np.square(t - mu).mean(-1, keepdims=True)
    return (t - mu) / np.sqrt(var + LN_EPS) * g + b


def setup_inputs():
    s = mx_kscale(DIN)
    x = bf(np.random.standard_normal((B, IN_DIM)) * s[MEM:])
    h = bf(np.random.standard_normal((B, MEM)) * s[:MEM])
    W1_words, W1_scales = pack_weight(np.random.standard_normal((DIN, F)) * 1.3 / np.sqrt(DIN) / s[:, None], FMT)
    b1 = bf(np.random.standard_normal(F) * 0.3)
    g1 = bf(1.0 + 0.1 * np.random.standard_normal(F))
    be1 = bf(np.random.standard_normal(F) * 0.2)
    W2_words, W2_scales = pack_weight(np.random.standard_normal((F, MEM)) / np.sqrt(F), FMT)
    b2 = bf(np.random.standard_normal(MEM) * 0.2)
    return {"x": x,
            "h": h,
            "W1_words": W1_words,
            "W1_scales": W1_scales,
            "b1": b1,
            "g1": g1,
            "be1": be1,
            "W2_words": W2_words,
            "W2_scales": W2_scales,
            "b2": b2}


def reference(x, h, W1_words, W1_scales, b1, g1, be1, W2_words, W2_scales, b2):
    combined = np.concatenate([f64(h), f64(x)], axis=-1)
    u = (mxq(combined, 1, "e4m3") @ unpack_weight(W1_words, W1_scales, FMT)) + f64(b1)
    t = gelu_erf(layernorm(u, f64(g1), f64(be1)))
    return np.tanh((mxq(t, 1, "e4m3") @ unpack_weight(W2_words, W2_scales, FMT)) + f64(b2))

@@ -1,0 +1,299 @@
+from contextlib import ExitStack
+
+import concourse.mybir as mybir
+from concourse.masks import make_identity
+
+F32 = mybir.dt.float32
+BF16 = mybir.dt.bfloat16
+I32 = mybir.dt.int32
+U32 = mybir.dt.uint32
+U8 = mybir.dt.uint8
+FP8X4 = mybir.dt.float8_e4m3fn_x4
+ALU = mybir.AluOpType
+ACT = mybir.ActivationFunctionType
+
+P = 128
+PACK = 4
+PAIRS = 2
+K_PASS = P * PACK
+BATCH, IN_DIM, MEM = 512, 16128, 256
+FEATURES = 2 * MEM
+N_GROUPS = (MEM + IN_DIM) // K_PASS
+M_TILES = BATCH // P
+LN_EPS = 1e-5
+
+CHUNK_GROUPS = (2, 2, 4, 8, 8, 8)
+GROUPS_PER_BANK = 2
+W_LOAD_GROUPS = 4
+PLANE_SLOTS = 8
+LOOKAHEAD = 5
+STEPS_AFTER = 3
+
+FLOPS = 2 * BATCH * (MEM + IN_DIM) * FEATURES + 2 * BATCH * FEATURES * MEM
+
+
+def tile_liquidmemorycell_pa_k_kernel(
+    tc, x, h, W1_words, W1_scales, b1, g1, be1, W2_words, W2_scales, b2, out
+):
+    nc = tc.nc
+
+    units = []
+    first_group = 0
+    for n_groups in CHUNK_GROUPS:
+        for m in range(M_TILES):
+            units.append((first_group, n_groups, m))
+        first_group += n_groups
+    assert first_group == N_GROUPS
+    n_units = len(units)
+
+    with ExitStack() as ctx:
+        const = ctx.enter_context(tc.tile_pool(name="const", bufs=1))
+        rows_pool = ctx.enter_context(tc.tile_pool(name="rows", bufs=LOOKAHEAD + 1))
+        sorted_pool = ctx.enter_context(tc.tile_pool(name="sorted", bufs=2))
+        grouped_pool = ctx.enter_context(tc.tile_pool(name="grouped", bufs=2))
+        codes_pool = ctx.enter_context(tc.tile_pool(name="codes", bufs=3))
+        tail_pool = ctx.enter_context(tc.tile_pool(name="tail", bufs=2))
+        acc_pool = ctx.enter_context(tc.psum_pool(name="acc", bufs=1))
+        bank_pool = ctx.enter_context(tc.psum_pool(name="banks", bufs=4))
+        ctx.enter_context(tc.manual_schedule())
+
+        w1_words = const.tile([P, N_GROUPS, FEATURES], U32, align_bytes=64)
+        w1_planes = const.tile([P, PLANE_SLOTS, FEATURES], U8, align_bytes=64)
+        w2_words = const.tile([P, MEM], U32, align_bytes=64)
+        w2_plane = const.tile([P, MEM], U8, align_bytes=64)
+        ident = const.tile([P, P], F32)
+        ones = const.tile([P, P], BF16)
+        bias_rows = const.tile([P, FEATURES + MEM], BF16)
+        b1_sorted = const.tile([P, PACK, P], F32)
+        b2_all = const.tile([P, MEM], F32)
+        g1_bf = const.tile([P, PACK], BF16)
+        be1_bf = const.tile([P, PACK], BF16)
+        g1_col = const.tile([P, PACK], F32)
+        be1_col = const.tile([P, PACK], F32)
+        neg_half = const.tile([P, 1], F32)
+        warm_in = const.tile([P, 1], F32)
+        warm_out = const.tile([P, 1], F32)
+        pre_tanh = const.tile([P, M_TILES, MEM], F32)
+        result = const.tile([P, M_TILES, MEM], F32)
+        acc = [acc_pool.tile([P, FEATURES], F32, name="acc%d" % m) for m in range(M_TILES)]
+
+        rows, pairs_sorted, codes, planes = {}, {}, {}, {}
+        shifted, mean_var, rstd, normed, t_codes, t_plane = {}, {}, {}, {}, {}, {}
+
+        def load_rows(i):
+            g0, n, m = units[i]
+            rows[i] = rows_pool.tile([P, n * K_PASS], BF16, name="rows")
+            batch = slice(m * P, (m + 1) * P)
+            if g0 == 0:
+                nc.sync.dma_start(out=rows[i][:, 0:MEM], in_=h[batch, :])
+                nc.sync.dma_start(out=rows[i][:, MEM:], in_=x[batch, 0 : n * K_PASS - MEM])
+            else:
+                first = g0 * K_PASS - MEM
+                nc.sync.dma_start(out=rows[i][:], in_=x[batch, first : first + n * K_PASS])
+
+        def load_w1_words(g0, n):
+            for g in range(g0, g0 + n, W_LOAD_GROUPS):
+                some = slice(g, min(g + W_LOAD_GROUPS, g0 + n))
+                nc.sync.dma_start(
+                    out=w1_words[:, some, :].bitcast(I32),
+                    in_=W1_words[some].rearrange("g p n t -> p g (n t)").bitcast(I32),
+                )
+
+        def load_w1_scales():
+            for j in range(N_GROUPS // PLANE_SLOTS):
+                for quadrant in range(4):
+                    first = 32 * quadrant + 4 * j
+                    nc.sync.dma_start(
+                        out=w1_planes[first : first + 4, :, :].bitcast(I32),
+                        in_=W1_scales[
+                            PLANE_SLOTS * j : PLANE_SLOTS * (j + 1), 4 * quadrant : 4 * quadrant + 4, :
+                        ]
+                        .rearrange("g r n -> r g n")
+                        .bitcast(I32),
+                    )
+
+        def load_w2():
+            nc.sync.dma_start(
+                out=w2_words[:].bitcast(I32),
+                in_=W2_words[0].rearrange("p n t -> p (n t)").bitcast(I32),
+            )
+            for quadrant in range(4):
+                nc.sync.dma_start(
+                    out=w2_plane[32 * quadrant : 32 * quadrant + 4, :].bitcast(I32),
+                    in_=W2_scales[0, 4 * quadrant : 4 * quadrant + 4, :].bitcast(I32),
+                )
+
+        def load_unit(i):
+            g0, n, m = units[i]
+            if m == 0:
+                load_w1_words(g0, n)
+            load_rows(i)
+
+        def sort_pairs(i):
+            g0, n, m = units[i]
+            pairs_sorted[i] = sorted_pool.tile([P, n, PAIRS, P], F32, name="pairs_sorted")
+            nc.vector.tensor_copy(
+                out=pairs_sorted[i][:],
+                in_=rows[i][:].bitcast(F32).rearrange("b (g p u) -> b g u p", p=P, u=PAIRS),
+            )
+
+        def transpose_unit(i):
+            g0, n, m = units[i]
+            grouped = grouped_pool.tile([P, n * P * PACK], BF16, name="grouped", align_bytes=64)
+            grouped_pairs = grouped[:].bitcast(F32).rearrange("p (g b u) -> p g b u", b=P, u=PAIRS)
+            for g in range(0, n, GROUPS_PER_BANK):
+                bank = bank_pool.tile([P, GROUPS_PER_BANK, PAIRS, P], F32, name="bank")
+                for gg in range(GROUPS_PER_BANK):
+                    for u in range(PAIRS):
+                        nc.tensor.transpose(
+                            out=bank[:, gg, u, :], in_=pairs_sorted[i][:, g + gg, u, :], identity=ident[:]
+                        )
+                nc.scalar.copy(
+                    out=grouped_pairs[:, g : g + GROUPS_PER_BANK, :, :],
+                    in_=bank[:].rearrange("p g u b -> p g b u"),
+                )
+            return grouped
+
+        def quantise_unit(i, grouped):
+            g0, n, m = units[i]
+            codes[i] = codes_pool.tile([P, n * P], U32, name="codes", align_bytes=64)
+            planes[i] = codes_pool.tile([P, n * P], U8, name="planes", align_bytes=64)
+            nc.vector.quantize_mx(out=codes[i][:].bitcast(FP8X4), scales=planes[i][:], in_=grouped[:])
+
+        def multiply_unit(i):
+            g0, n, m = units[i]
+            for gi in range(n):
+                g = g0 + gi
+                cols = slice(gi * P, (gi + 1) * P)
+                nc.tensor.matmul_mx(
+                    out=acc[m][:],
+                    lhsT=codes[i][:, cols].bitcast(FP8X4),
+                    lhsT_scale=planes[i][:, cols],
+                    rhs=w1_words[:, g, :].bitcast(FP8X4),
+                    rhs_scale=w1_planes[4 * (g // PLANE_SLOTS) : P, g % PLANE_SLOTS, :],
+                    start=(g == 0),
+                    stop=(g == N_GROUPS - 1),
+                )
+
+        def statistics(m):
+            shifted[m] = tail_pool.tile([P, PACK, P], F32, name="shifted")
+            nc.vector.tensor_tensor(
+                out=shifted[m][:],
+                in0=acc[m][:].rearrange("b (p t) -> b t p", t=PACK),
+                in1=b1_sorted[:],
+                op=ALU.add,
+            )
+            stats = tail_pool.tile([P, 6], F32, name="stats")
+            nc.vector.bn_stats(out=stats[:], in_=shifted[m][:].rearrange("b t p -> b (t p)"))
+            mean_var[m] = tail_pool.tile([P, 2], F32, name="mean_var")
+            nc.vector.bn_aggr(out=mean_var[m][:], in_=stats[:])
+            var_eps = tail_pool.tile([P, 1], F32, name="var_eps")
+            nc.vector.tensor_scalar_add(out=var_eps[:], in0=mean_var[m][:, 1:2], scalar1=LN_EPS)
+            rstd[m] = tail_pool.tile([P, 1], F32, name="rstd")
+            nc.gpsimd.tensor_tensor(out=rstd[m][:], in0=var_eps[:], in1=neg_half[:], op=ALU.pow)
+
+        def normalise(m):
+            normed[m] = tail_pool.tile([P, PACK, P], F32, name="normed")
+            nc.vector.tensor_scalar(
+                out=normed[m][:],
+                in0=shifted[m][:],
+                scalar1=mean_var[m][:, 0:1],
+                scalar2=rstd[m][:],
+                op0=ALU.subtract,
+                op1=ALU.mult,
+            )
+
+        def gelu_and_quantise(m):
+            flipped = acc_pool.tile([P, PACK, P], F32, name="flipped%d" % m, tag="acc%d" % m)
+            t_planes = tail_pool.tile([P, PACK, P], BF16, name="t_planes")
+            for t in range(PACK):
+                nc.tensor.transpose(out=flipped[:, t, :], in_=normed[m][:, t, :], identity=ident[:])
+            for t in range(PACK):
+                nc.scalar.activation(
+                    out=t_planes[:, t, :],
+                    in_=flipped[:, t, :],
+                    func=ACT.Gelu,
+                    bias=be1_col[:, t : t + 1],
+                    scale=g1_col[:, t : t + 1],
+                )
+            t_grouped = tail_pool.tile([P, P, PACK], BF16, name="t_grouped", align_bytes=64)
+            nc.vector.tensor_copy(out=t_grouped[:], in_=t_planes[:].rearrange("p t b -> p b t"))
+            t_codes[m] = tail_pool.tile([P, P], U32, name="t_codes", align_bytes=64)
+            t_plane[m] = tail_pool.tile([P, P], U8, name="t_plane", align_bytes=64)
+            nc.vector.quantize_mx(
+                out=t_codes[m][:].bitcast(FP8X4),
+                scales=t_plane[m][:],
+                in_=t_grouped[:].rearrange("p b t -> p (b t)"),
+            )
+
+        def second_product(m):
+            product = acc_pool.tile([P, MEM], F32, name="product%d" % m, tag="acc%d" % m)
+            nc.tensor.matmul_mx(
+                out=product[:],
+                lhsT=t_codes[m][:].bitcast(FP8X4),
+                lhsT_scale=t_plane[m][:],
+                rhs=w2_words[:].bitcast(FP8X4),
+                rhs_scale=w2_plane[:],
+                start=True,
+                stop=True,
+            )
+            nc.vector.tensor_tensor(out=pre_tanh[:, m, :], in0=product[:], in1=b2_all[:], op=ALU.add)
+
+        nc.vector.memset(w1_planes[:].rearrange("p s n -> p (s n)").bitcast(I32), 0)
+        nc.vector.memset(w2_plane[:].bitcast(I32), 0)
+        nc.vector.memset(warm_in[:], 0.0)
+        nc.gpsimd.memset(bias_rows[:], 0.0)
+        nc.gpsimd.memset(ones[:], 1.0)
+        nc.gpsimd.memset(neg_half[:], -0.5)
+        make_identity(nc, ident[:])
+
+        nc.scalar.dma_start(out=bias_rows[0:1, 0:FEATURES], in_=b1.unsqueeze(0))
+        nc.scalar.dma_start(out=bias_rows[0:1, FEATURES:], in_=b2.unsqueeze(0))
+        nc.scalar.dma_start(out=g1_bf[:], in_=g1.rearrange("(p t) -> p t", t=PACK))
+        nc.scalar.dma_start(out=be1_bf[:], in_=be1.rearrange("(p t) -> p t", t=PACK))
+        nc.scalar.activation(out=warm_out[:], in_=warm_in[:], func=ACT.Gelu)
+
+        load_rows(0)
+        load_w1_scales()
+        load_w1_words(units[0][0], units[0][1])
+        for i in range(1, LOOKAHEAD):
+            load_unit(i)
+        load_w2()
+
+        nc.gpsimd.tensor_copy(out=g1_col[:], in_=g1_bf[:])
+        nc.gpsimd.tensor_copy(out=be1_col[:], in_=be1_bf[:])
+
+        b1_bank = bank_pool.tile([P, FEATURES], F32, name="b1_bank", tag="bank")
+        nc.tensor.matmul(out=b1_bank[:], lhsT=ones[:], rhs=bias_rows[:, 0:FEATURES], start=True, stop=True)
+        nc.scalar.copy(out=b1_sorted[:], in_=b1_bank[:].rearrange("b (p t) -> b t p", t=PACK))
+        b2_bank = bank_pool.tile([P, MEM], F32, name="b2_bank", tag="bank")
+        nc.tensor.matmul(out=b2_bank[:], lhsT=ones[:], rhs=bias_rows[:, FEATURES:], start=True, stop=True)
+        nc.scalar.copy(out=b2_all[:], in_=b2_bank[:])
+
+        def is_tile(m):
+            return 0 <= m < M_TILES
+
+        first_done = n_units - M_TILES + 1
+        sort_pairs(0)
+        for i in range(n_units + STEPS_AFTER + 1):
+            done = i - first_done
+            if i + LOOKAHEAD < n_units:
+                load_unit(i + LOOKAHEAD)
+            if i + 1 < n_units:
+                sort_pairs(i + 1)
+            if is_tile(done - 1):
+                normalise(done - 1)
+            if is_tile(done - 2):
+                gelu_and_quantise(done - 2)
+            if i < n_units:
+                quantise_unit(i, transpose_unit(i))
+            if 1 <= i <= n_units:
+                multiply_unit(i - 1)
+            if is_tile(done - 3):
+                second_product(done - 3)
+            if is_tile(done):
+                statistics(done)
+
+        for m in range(M_TILES):
+            nc.scalar.activation(out=result[:, m, :], in_=pre_tanh[:, m, :], func=ACT.Tanh)
+            nc.sync.dma_start(out=out[m * P : (m + 1) * P, :], in_=result[:, m, :])

@@ -23,11 +23,12 @@ M_TILES = BATCH // P
 LN_EPS = 1e-5
 
 CHUNK_GROUPS = (2, 2, 4, 8, 8, 8)
+UNIT_GROUPS = 4
 GROUPS_PER_BANK = 2
-W_LOAD_GROUPS = 4
 PLANE_SLOTS = 8
-LOOKAHEAD = 5
-STEPS_AFTER = 3
+LOOKAHEAD = 8
+LAG = 2
+NORMALISE_AT, GELU_AT, SECOND_AT = 1, 3, 5
 
 FLOPS = 2 * BATCH * (MEM + IN_DIM) * FEATURES + 2 * BATCH * FEATURES * MEM
 
@@ -41,17 +42,27 @@ def tile_liquidmemorycell_pa_k_kernel(
     first_group = 0
     for n_groups in CHUNK_GROUPS:
         for m in range(M_TILES):
-            units.append((first_group, n_groups, m))
+            for g in range(first_group, first_group + n_groups, UNIT_GROUPS):
+                units.append((g, min(UNIT_GROUPS, n_groups), m))
         first_group += n_groups
     assert first_group == N_GROUPS
     n_units = len(units)
+    chunk_of = {}
+    first_group = 0
+    for n_groups in CHUNK_GROUPS:
+        chunk_of[(first_group, 0)] = n_groups
+        first_group += n_groups
+    completes = {}
+    for i in range(n_units):
+        if units[i][0] + units[i][1] == N_GROUPS:
+            completes[i + LAG] = units[i][2]
 
     with ExitStack() as ctx:
         const = ctx.enter_context(tc.tile_pool(name="const", bufs=1))
         rows_pool = ctx.enter_context(tc.tile_pool(name="rows", bufs=LOOKAHEAD + 1))
-        sorted_pool = ctx.enter_context(tc.tile_pool(name="sorted", bufs=2))
-        grouped_pool = ctx.enter_context(tc.tile_pool(name="grouped", bufs=2))
-        codes_pool = ctx.enter_context(tc.tile_pool(name="codes", bufs=3))
+        sorted_pool = ctx.enter_context(tc.tile_pool(name="sorted", bufs=3))
+        grouped_pool = ctx.enter_context(tc.tile_pool(name="grouped", bufs=3))
+        codes_pool = ctx.enter_context(tc.tile_pool(name="codes", bufs=LAG + 2))
         tail_pool = ctx.enter_context(tc.tile_pool(name="tail", bufs=2))
         acc_pool = ctx.enter_context(tc.psum_pool(name="acc", bufs=1))
         bank_pool = ctx.enter_context(tc.psum_pool(name="banks", bufs=4))
@@ -92,25 +103,24 @@ def tile_liquidmemorycell_pa_k_kernel(
                 nc.sync.dma_start(out=rows[i][:], in_=x[batch, first : first + n * K_PASS])
 
         def load_w1_words(g0, n):
-            for g in range(g0, g0 + n, W_LOAD_GROUPS):
-                some = slice(g, min(g + W_LOAD_GROUPS, g0 + n))
+            for g in range(g0, g0 + n, UNIT_GROUPS):
+                some = slice(g, min(g + UNIT_GROUPS, g0 + n))
                 nc.sync.dma_start(
                     out=w1_words[:, some, :].bitcast(I32),
                     in_=W1_words[some].rearrange("g p n t -> p g (n t)").bitcast(I32),
                 )
 
-        def load_w1_scales():
-            for j in range(N_GROUPS // PLANE_SLOTS):
-                for quadrant in range(4):
-                    first = 32 * quadrant + 4 * j
-                    nc.sync.dma_start(
-                        out=w1_planes[first : first + 4, :, :].bitcast(I32),
-                        in_=W1_scales[
-                            PLANE_SLOTS * j : PLANE_SLOTS * (j + 1), 4 * quadrant : 4 * quadrant + 4, :
-                        ]
-                        .rearrange("g r n -> r g n")
-                        .bitcast(I32),
-                    )
+        def load_w1_scales(j, queue, view):
+            for quadrant in range(4):
+                first = 32 * quadrant + 4 * j
+                queue.dma_start(
+                    out=w1_planes[first : first + 4, :, :].bitcast(view),
+                    in_=W1_scales[
+                        PLANE_SLOTS * j : PLANE_SLOTS * (j + 1), 4 * quadrant : 4 * quadrant + 4, :
+                    ]
+                    .rearrange("g r n -> r g n")
+                    .bitcast(view),
+                )
 
         def load_w2():
             nc.sync.dma_start(
@@ -125,8 +135,8 @@ def tile_liquidmemorycell_pa_k_kernel(
 
         def load_unit(i):
             g0, n, m = units[i]
-            if m == 0:
-                load_w1_words(g0, n)
+            if (g0, m) in chunk_of:
+                load_w1_words(g0, chunk_of[(g0, m)])
             load_rows(i)
 
         def sort_pairs(i):
@@ -238,6 +248,8 @@ def tile_liquidmemorycell_pa_k_kernel(
                 stop=True,
             )
             nc.vector.tensor_tensor(out=pre_tanh[:, m, :], in0=product[:], in1=b2_all[:], op=ALU.add)
+            nc.scalar.activation(out=result[:, m, :], in_=pre_tanh[:, m, :], func=ACT.Tanh)
+            nc.sync.dma_start(out=out[m * P : (m + 1) * P, :], in_=result[:, m, :])
 
         nc.vector.memset(w1_planes[:].rearrange("p s n -> p (s n)").bitcast(I32), 0)
         nc.vector.memset(w2_plane[:].bitcast(I32), 0)
@@ -254,11 +266,13 @@ def tile_liquidmemorycell_pa_k_kernel(
         nc.scalar.activation(out=warm_out[:], in_=warm_in[:], func=ACT.Gelu)
 
         load_rows(0)
-        load_w1_scales()
-        load_w1_words(units[0][0], units[0][1])
+        load_w1_scales(0, nc.sync, I32)
+        load_w1_words(0, CHUNK_GROUPS[0])
         for i in range(1, LOOKAHEAD):
             load_unit(i)
         load_w2()
+        for j in range(1, N_GROUPS // PLANE_SLOTS):
+            load_w1_scales(j, nc.gpsimd, F32)
 
         nc.gpsimd.tensor_copy(out=g1_col[:], in_=g1_bf[:])
         nc.gpsimd.tensor_copy(out=be1_col[:], in_=be1_bf[:])
@@ -270,30 +284,21 @@ def tile_liquidmemorycell_pa_k_kernel(
         nc.tensor.matmul(out=b2_bank[:], lhsT=ones[:], rhs=bias_rows[:, FEATURES:], start=True, stop=True)
         nc.scalar.copy(out=b2_all[:], in_=b2_bank[:])
 
-        def is_tile(m):
-            return 0 <= m < M_TILES
-
-        first_done = n_units - M_TILES + 1
         sort_pairs(0)
-        for i in range(n_units + STEPS_AFTER + 1):
-            done = i - first_done
+        for i in range(n_units + LAG + SECOND_AT):
             if i + LOOKAHEAD < n_units:
                 load_unit(i + LOOKAHEAD)
             if i + 1 < n_units:
                 sort_pairs(i + 1)
-            if is_tile(done - 1):
-                normalise(done - 1)
-            if is_tile(done - 2):
-                gelu_and_quantise(done - 2)
+            if i - GELU_AT in completes:
+                gelu_and_quantise(completes[i - GELU_AT])
             if i < n_units:
                 quantise_unit(i, transpose_unit(i))
-            if 1 <= i <= n_units:
-                multiply_unit(i - 1)
-            if is_tile(done - 3):
-                second_product(done - 3)
-            if is_tile(done):
-                statistics(done)
-
-        for m in range(M_TILES):
-            nc.scalar.activation(out=result[:, m, :], in_=pre_tanh[:, m, :], func=ACT.Tanh)
-            nc.sync.dma_start(out=out[m * P : (m + 1) * P, :], in_=result[:, m, :])
+            if LAG <= i < n_units + LAG:
+                multiply_unit(i - LAG)
+            if i - SECOND_AT in completes:
+                second_product(completes[i - SECOND_AT])
+            if i - NORMALISE_AT in completes:
+                normalise(completes[i - NORMALISE_AT])
+            if i in completes:
+                statistics(completes[i])

@@ -22,11 +22,13 @@ N_GROUPS = (MEM + IN_DIM) // K_PASS
 M_TILES = BATCH // P
 LN_EPS = 1e-5
 
-CHUNK_GROUPS = (2, 2, 4, 8, 8, 8)
 UNIT_GROUPS = 4
+UNIT_COLS = UNIT_GROUPS * K_PASS
 GROUPS_PER_BANK = 2
+CHUNK_GROUPS = (4, 4, 8, 8, 8)
 PLANE_SLOTS = 8
 LOOKAHEAD = 8
+SORT_AHEAD = 2
 LAG = 2
 NORMALISE_AT, GELU_AT, SECOND_AT = 1, 3, 5
 
@@ -43,24 +45,20 @@ def tile_liquidmemorycell_pa_k_kernel(
     for n_groups in CHUNK_GROUPS:
         for m in range(M_TILES):
             for g in range(first_group, first_group + n_groups, UNIT_GROUPS):
-                units.append((g, min(UNIT_GROUPS, n_groups), m))
+                units.append((g, m))
         first_group += n_groups
     assert first_group == N_GROUPS
     n_units = len(units)
-    chunk_of = {}
-    first_group = 0
-    for n_groups in CHUNK_GROUPS:
-        chunk_of[(first_group, 0)] = n_groups
-        first_group += n_groups
+    half_way = n_units // 2
     completes = {}
     for i in range(n_units):
-        if units[i][0] + units[i][1] == N_GROUPS:
-            completes[i + LAG] = units[i][2]
+        if units[i][0] + UNIT_GROUPS == N_GROUPS:
+            completes[i + LAG] = units[i][1]
 
     with ExitStack() as ctx:
         const = ctx.enter_context(tc.tile_pool(name="const", bufs=1))
         rows_pool = ctx.enter_context(tc.tile_pool(name="rows", bufs=LOOKAHEAD + 1))
-        sorted_pool = ctx.enter_context(tc.tile_pool(name="sorted", bufs=3))
+        sorted_pool = ctx.enter_context(tc.tile_pool(name="sorted", bufs=SORT_AHEAD + 2))
         grouped_pool = ctx.enter_context(tc.tile_pool(name="grouped", bufs=3))
         codes_pool = ctx.enter_context(tc.tile_pool(name="codes", bufs=LAG + 2))
         tail_pool = ctx.enter_context(tc.tile_pool(name="tail", bufs=2))
@@ -92,37 +90,38 @@ def tile_liquidmemorycell_pa_k_kernel(
         shifted, mean_var, rstd, normed, t_codes, t_plane = {}, {}, {}, {}, {}, {}
 
         def load_rows(i):
-            g0, n, m = units[i]
-            rows[i] = rows_pool.tile([P, n * K_PASS], BF16, name="rows")
+            g0, m = units[i]
+            rows[i] = rows_pool.tile([P, UNIT_COLS], BF16, name="rows")
             batch = slice(m * P, (m + 1) * P)
             if g0 == 0:
                 nc.sync.dma_start(out=rows[i][:, 0:MEM], in_=h[batch, :])
-                nc.sync.dma_start(out=rows[i][:, MEM:], in_=x[batch, 0 : n * K_PASS - MEM])
+                nc.sync.dma_start(out=rows[i][:, MEM:], in_=x[batch, 0 : UNIT_COLS - MEM])
             else:
                 first = g0 * K_PASS - MEM
-                nc.sync.dma_start(out=rows[i][:], in_=x[batch, first : first + n * K_PASS])
+                nc.sync.dma_start(out=rows[i][:], in_=x[batch, first : first + UNIT_COLS])
 
-        def load_w1_words(g0, n):
-            for g in range(g0, g0 + n, UNIT_GROUPS):
-                some = slice(g, min(g + UNIT_GROUPS, g0 + n))
-                nc.sync.dma_start(
-                    out=w1_words[:, some, :].bitcast(I32),
-                    in_=W1_words[some].rearrange("g p n t -> p g (n t)").bitcast(I32),
-                )
+        def load_w1(g0):
+            if g0 % PLANE_SLOTS == 0:
+                j = g0 // PLANE_SLOTS
+                for quadrant in range(4):
+                    first = 32 * quadrant + 4 * j
+                    nc.sync.dma_start(
+                        out=w1_planes[first : first + 4, :, :].bitcast(I32),
+                        in_=W1_scales[g0 : g0 + PLANE_SLOTS, 4 * quadrant : 4 * quadrant + 4, :]
+                        .rearrange("g r n -> r g n")
+                        .bitcast(I32),
+                    )
+            some = slice(g0, g0 + UNIT_GROUPS)
+            nc.sync.dma_start(
+                out=w1_words[:, some, :].bitcast(I32),
+                in_=W1_words[some].rearrange("g p n t -> p g (n t)").bitcast(I32),
+            )
 
-        def load_w1_scales(j, queue, view):
-            for quadrant in range(4):
-                first = 32 * quadrant + 4 * j
-                queue.dma_start(
-                    out=w1_planes[first : first + 4, :, :].bitcast(view),
-                    in_=W1_scales[
-                        PLANE_SLOTS * j : PLANE_SLOTS * (j + 1), 4 * quadrant : 4 * quadrant + 4, :
-                    ]
-                    .rearrange("g r n -> r g n")
-                    .bitcast(view),
-                )
-
-        def load_w2():
+        def load_small():
+            nc.sync.dma_start(out=bias_rows[0:1, 0:FEATURES], in_=b1.unsqueeze(0))
+            nc.sync.dma_start(out=bias_rows[0:1, FEATURES:], in_=b2.unsqueeze(0))
+            nc.sync.dma_start(out=g1_bf[:], in_=g1.rearrange("(p t) -> p t", t=PACK))
+            nc.sync.dma_start(out=be1_bf[:], in_=be1.rearrange("(p t) -> p t", t=PACK))
             nc.sync.dma_start(
                 out=w2_words[:].bitcast(I32),
                 in_=W2_words[0].rearrange("p n t -> p (n t)").bitcast(I32),
@@ -133,25 +132,24 @@ def tile_liquidmemorycell_pa_k_kernel(
                     in_=W2_scales[0, 4 * quadrant : 4 * quadrant + 4, :].bitcast(I32),
                 )
 
-        def load_unit(i):
-            g0, n, m = units[i]
-            if (g0, m) in chunk_of:
-                load_w1_words(g0, chunk_of[(g0, m)])
+        def request(i):
             load_rows(i)
+            if i >= LAG and units[i - LAG][1] == 0:
+                load_w1(units[i - LAG][0])
+            if i == half_way:
+                load_small()
 
         def sort_pairs(i):
-            g0, n, m = units[i]
-            pairs_sorted[i] = sorted_pool.tile([P, n, PAIRS, P], F32, name="pairs_sorted")
+            pairs_sorted[i] = sorted_pool.tile([P, UNIT_GROUPS, PAIRS, P], F32, name="pairs_sorted")
             nc.vector.tensor_copy(
                 out=pairs_sorted[i][:],
                 in_=rows[i][:].bitcast(F32).rearrange("b (g p u) -> b g u p", p=P, u=PAIRS),
             )
 
         def transpose_unit(i):
-            g0, n, m = units[i]
-            grouped = grouped_pool.tile([P, n * P * PACK], BF16, name="grouped", align_bytes=64)
+            grouped = grouped_pool.tile([P, UNIT_GROUPS * P * PACK], BF16, name="grouped", align_bytes=64)
             grouped_pairs = grouped[:].bitcast(F32).rearrange("p (g b u) -> p g b u", b=P, u=PAIRS)
-            for g in range(0, n, GROUPS_PER_BANK):
+            for g in range(0, UNIT_GROUPS, GROUPS_PER_BANK):
                 bank = bank_pool.tile([P, GROUPS_PER_BANK, PAIRS, P], F32, name="bank")
                 for gg in range(GROUPS_PER_BANK):
                     for u in range(PAIRS):
@@ -165,14 +163,13 @@ def tile_liquidmemorycell_pa_k_kernel(
             return grouped
 
         def quantise_unit(i, grouped):
-            g0, n, m = units[i]
-            codes[i] = codes_pool.tile([P, n * P], U32, name="codes", align_bytes=64)
-            planes[i] = codes_pool.tile([P, n * P], U8, name="planes", align_bytes=64)
+            codes[i] = codes_pool.tile([P, UNIT_GROUPS * P], U32, name="codes", align_bytes=64)
+            planes[i] = codes_pool.tile([P, UNIT_GROUPS * P], U8, name="planes", align_bytes=64)
             nc.vector.quantize_mx(out=codes[i][:].bitcast(FP8X4), scales=planes[i][:], in_=grouped[:])
 
         def multiply_unit(i):
-            g0, n, m = units[i]
-            for gi in range(n):
+            g0, m = units[i]
+            for gi in range(UNIT_GROUPS):
                 g = g0 + gi
                 cols = slice(gi * P, (gi + 1) * P)
                 nc.tensor.matmul_mx(
@@ -184,6 +181,16 @@ def tile_liquidmemorycell_pa_k_kernel(
                     start=(g == 0),
                     stop=(g == N_GROUPS - 1),
                 )
+
+        def broadcast_biases():
+            b1_bank = bank_pool.tile([P, FEATURES], F32, name="b1_bank", tag="bank")
+            nc.tensor.matmul(out=b1_bank[:], lhsT=ones[:], rhs=bias_rows[:, 0:FEATURES], start=True, stop=True)
+            nc.scalar.copy(out=b1_sorted[:], in_=b1_bank[:].rearrange("b (p t) -> b t p", t=PACK))
+            b2_bank = bank_pool.tile([P, MEM], F32, name="b2_bank", tag="bank")
+            nc.tensor.matmul(out=b2_bank[:], lhsT=ones[:], rhs=bias_rows[:, FEATURES:], start=True, stop=True)
+            nc.scalar.copy(out=b2_all[:], in_=b2_bank[:])
+            nc.gpsimd.tensor_copy(out=g1_col[:], in_=g1_bf[:])
+            nc.gpsimd.tensor_copy(out=be1_col[:], in_=be1_bf[:])
 
         def statistics(m):
             shifted[m] = tail_pool.tile([P, PACK, P], F32, name="shifted")
@@ -254,48 +261,30 @@ def tile_liquidmemorycell_pa_k_kernel(
         nc.vector.memset(w1_planes[:].rearrange("p s n -> p (s n)").bitcast(I32), 0)
         nc.vector.memset(w2_plane[:].bitcast(I32), 0)
         nc.vector.memset(warm_in[:], 0.0)
+        make_identity(nc, ident[:])
         nc.gpsimd.memset(bias_rows[:], 0.0)
         nc.gpsimd.memset(ones[:], 1.0)
         nc.gpsimd.memset(neg_half[:], -0.5)
-        make_identity(nc, ident[:])
-
-        nc.scalar.dma_start(out=bias_rows[0:1, 0:FEATURES], in_=b1.unsqueeze(0))
-        nc.scalar.dma_start(out=bias_rows[0:1, FEATURES:], in_=b2.unsqueeze(0))
-        nc.scalar.dma_start(out=g1_bf[:], in_=g1.rearrange("(p t) -> p t", t=PACK))
-        nc.scalar.dma_start(out=be1_bf[:], in_=be1.rearrange("(p t) -> p t", t=PACK))
         nc.scalar.activation(out=warm_out[:], in_=warm_in[:], func=ACT.Gelu)
 
-        load_rows(0)
-        load_w1_scales(0, nc.sync, I32)
-        load_w1_words(0, CHUNK_GROUPS[0])
-        for i in range(1, LOOKAHEAD):
-            load_unit(i)
-        load_w2()
-        for j in range(1, N_GROUPS // PLANE_SLOTS):
-            load_w1_scales(j, nc.gpsimd, F32)
+        for i in range(LOOKAHEAD):
+            request(i)
+        for i in range(SORT_AHEAD):
+            sort_pairs(i)
 
-        nc.gpsimd.tensor_copy(out=g1_col[:], in_=g1_bf[:])
-        nc.gpsimd.tensor_copy(out=be1_col[:], in_=be1_bf[:])
-
-        b1_bank = bank_pool.tile([P, FEATURES], F32, name="b1_bank", tag="bank")
-        nc.tensor.matmul(out=b1_bank[:], lhsT=ones[:], rhs=bias_rows[:, 0:FEATURES], start=True, stop=True)
-        nc.scalar.copy(out=b1_sorted[:], in_=b1_bank[:].rearrange("b (p t) -> b t p", t=PACK))
-        b2_bank = bank_pool.tile([P, MEM], F32, name="b2_bank", tag="bank")
-        nc.tensor.matmul(out=b2_bank[:], lhsT=ones[:], rhs=bias_rows[:, FEATURES:], start=True, stop=True)
-        nc.scalar.copy(out=b2_all[:], in_=b2_bank[:])
-
-        sort_pairs(0)
         for i in range(n_units + LAG + SECOND_AT):
             if i + LOOKAHEAD < n_units:
-                load_unit(i + LOOKAHEAD)
-            if i + 1 < n_units:
-                sort_pairs(i + 1)
+                request(i + LOOKAHEAD)
+            if i + SORT_AHEAD < n_units:
+                sort_pairs(i + SORT_AHEAD)
             if i - GELU_AT in completes:
                 gelu_and_quantise(completes[i - GELU_AT])
             if i < n_units:
                 quantise_unit(i, transpose_unit(i))
             if LAG <= i < n_units + LAG:
                 multiply_unit(i - LAG)
+            if i == half_way:
+                broadcast_biases()
             if i - SECOND_AT in completes:
                 second_product(completes[i - SECOND_AT])
             if i - NORMALISE_AT in completes:

@@ -26,7 +26,7 @@ UNIT_GROUPS = 4
 UNIT_COLS = UNIT_GROUPS * K_PASS
 GROUPS_PER_BANK = 2
 CHUNK_GROUPS = (4, 4, 8, 8, 8)
-PLANE_SLOTS = 8
+PLANE_GROUPS = 8
 LOOKAHEAD = 8
 SORT_AHEAD = 2
 LAG = 2
@@ -67,7 +67,10 @@ def tile_liquidmemorycell_pa_k_kernel(
         ctx.enter_context(tc.manual_schedule())
 
         w1_words = const.tile([P, N_GROUPS, FEATURES], U32, align_bytes=64)
-        w1_planes = const.tile([P, PLANE_SLOTS, FEATURES], U8, align_bytes=64)
+        w1_planes = [
+            const.tile([P, PLANE_GROUPS, FEATURES], U8, name="w1_planes%d" % j, align_bytes=64)
+            for j in range(N_GROUPS // PLANE_GROUPS)
+        ]
         w2_words = const.tile([P, MEM], U32, align_bytes=64)
         w2_plane = const.tile([P, MEM], U8, align_bytes=64)
         ident = const.tile([P, P], F32)
@@ -101,13 +104,11 @@ def tile_liquidmemorycell_pa_k_kernel(
                 nc.sync.dma_start(out=rows[i][:], in_=x[batch, first : first + UNIT_COLS])
 
         def load_w1(g0):
-            if g0 % PLANE_SLOTS == 0:
-                j = g0 // PLANE_SLOTS
+            if g0 % PLANE_GROUPS == 0:
                 for quadrant in range(4):
-                    first = 32 * quadrant + 4 * j
                     nc.sync.dma_start(
-                        out=w1_planes[first : first + 4, :, :].bitcast(I32),
-                        in_=W1_scales[g0 : g0 + PLANE_SLOTS, 4 * quadrant : 4 * quadrant + 4, :]
+                        out=w1_planes[g0 // PLANE_GROUPS][32 * quadrant : 32 * quadrant + 4, :, :].bitcast(I32),
+                        in_=W1_scales[g0 : g0 + PLANE_GROUPS, 4 * quadrant : 4 * quadrant + 4, :]
                         .rearrange("g r n -> r g n")
                         .bitcast(I32),
                     )
@@ -177,7 +178,7 @@ def tile_liquidmemorycell_pa_k_kernel(
                     lhsT=codes[i][:, cols].bitcast(FP8X4),
                     lhsT_scale=planes[i][:, cols],
                     rhs=w1_words[:, g, :].bitcast(FP8X4),
-                    rhs_scale=w1_planes[4 * (g // PLANE_SLOTS) : P, g % PLANE_SLOTS, :],
+                    rhs_scale=w1_planes[g // PLANE_GROUPS][:, g % PLANE_GROUPS, :],
                     start=(g == 0),
                     stop=(g == N_GROUPS - 1),
                 )
@@ -258,7 +259,8 @@ def tile_liquidmemorycell_pa_k_kernel(
             nc.scalar.activation(out=result[:, m, :], in_=pre_tanh[:, m, :], func=ACT.Tanh)
             nc.sync.dma_start(out=out[m * P : (m + 1) * P, :], in_=result[:, m, :])
 
-        nc.vector.memset(w1_planes[:].rearrange("p s n -> p (s n)").bitcast(I32), 0)
+        for plane_tile in w1_planes:
+            nc.vector.memset(plane_tile[:].rearrange("p g n -> p (g n)").bitcast(I32), 0)
         nc.vector.memset(w2_plane[:].bitcast(I32), 0)
         nc.vector.memset(warm_in[:], 0.0)
         make_identity(nc, ident[:])

@@ -26,7 +26,8 @@ UNIT_GROUPS = 4
 UNIT_COLS = UNIT_GROUPS * K_PASS
 GROUPS_PER_BANK = 2
 CHUNK_GROUPS = (4, 4, 8, 8, 8)
-PLANE_GROUPS = 8
+PLANE_GROUPS = 4
+PLANE_ROWS = 4
 LOOKAHEAD = 8
 SORT_AHEAD = 2
 LAG = 2
@@ -68,7 +69,7 @@ def tile_liquidmemorycell_pa_k_kernel(
 
         w1_words = const.tile([P, N_GROUPS, FEATURES], U32, align_bytes=64)
         w1_planes = [
-            const.tile([P, PLANE_GROUPS, FEATURES], U8, name="w1_planes%d" % j, align_bytes=64)
+            const.tile([P, FEATURES], U8, name="w1_planes%d" % j, align_bytes=64)
             for j in range(N_GROUPS // PLANE_GROUPS)
         ]
         w2_words = const.tile([P, MEM], U32, align_bytes=64)
@@ -104,14 +105,11 @@ def tile_liquidmemorycell_pa_k_kernel(
                 nc.sync.dma_start(out=rows[i][:], in_=x[batch, first : first + UNIT_COLS])
 
         def load_w1(g0):
-            if g0 % PLANE_GROUPS == 0:
-                for quadrant in range(4):
-                    nc.sync.dma_start(
-                        out=w1_planes[g0 // PLANE_GROUPS][32 * quadrant : 32 * quadrant + 4, :, :].bitcast(I32),
-                        in_=W1_scales[g0 : g0 + PLANE_GROUPS, 4 * quadrant : 4 * quadrant + 4, :]
-                        .rearrange("g r n -> r g n")
-                        .bitcast(I32),
-                    )
+            for quadrant in range(4):
+                nc.sync.dma_start(
+                    out=w1_planes[g0 // PLANE_GROUPS][32 * quadrant : 32 * quadrant + 16, :].bitcast(I32),
+                    in_=W1_scales[g0 : g0 + PLANE_GROUPS, 4 * quadrant : 4 * quadrant + 4, :].bitcast(I32),
+                )
             some = slice(g0, g0 + UNIT_GROUPS)
             nc.sync.dma_start(
                 out=w1_words[:, some, :].bitcast(I32),
@@ -178,7 +176,7 @@ def tile_liquidmemorycell_pa_k_kernel(
                     lhsT=codes[i][:, cols].bitcast(FP8X4),
                     lhsT_scale=planes[i][:, cols],
                     rhs=w1_words[:, g, :].bitcast(FP8X4),
-                    rhs_scale=w1_planes[g // PLANE_GROUPS][:, g % PLANE_GROUPS, :],
+                    rhs_scale=w1_planes[g // PLANE_GROUPS][PLANE_ROWS * (g % PLANE_GROUPS) :, :],
                     start=(g == 0),
                     stop=(g == N_GROUPS - 1),
                 )
@@ -260,7 +258,7 @@ def tile_liquidmemorycell_pa_k_kernel(
             nc.sync.dma_start(out=out[m * P : (m + 1) * P, :], in_=result[:, m, :])
 
         for plane_tile in w1_planes:
-            nc.vector.memset(plane_tile[:].rearrange("p g n -> p (g n)").bitcast(I32), 0)
+            nc.vector.memset(plane_tile[:].bitcast(I32), 0)
         nc.vector.memset(w2_plane[:].bitcast(I32), 0)
         nc.vector.memset(warm_in[:], 0.0)
         make_identity(nc, ident[:])

@@ -22,16 +22,16 @@ N_GROUPS = (MEM + IN_DIM) // K_PASS
 M_TILES = BATCH // P
 LN_EPS = 1e-5
 
-UNIT_GROUPS = 4
-UNIT_COLS = UNIT_GROUPS * K_PASS
 GROUPS_PER_BANK = 2
-CHUNK_GROUPS = (4, 4, 8, 8, 8)
+UNIT_GROUPS = 4
+CHUNKS = ((2, 2), (0, 2)) + tuple((g, 4) for g in range(4, N_GROUPS, 4))
+RUN_GROUPS = 8
+SINGLE_CHUNKS = (0, 1, 2, len(CHUNKS) - 1)
 PLANE_GROUPS = 4
 PLANE_ROWS = 4
-LOOKAHEAD = 8
+LOOKAHEAD = 10
 SORT_AHEAD = 2
-LAG = 2
-NORMALISE_AT, GELU_AT, SECOND_AT = 1, 3, 5
+W1_BEHIND = 2
 
 FLOPS = 2 * BATCH * (MEM + IN_DIM) * FEATURES + 2 * BATCH * FEATURES * MEM
 
@@ -42,26 +42,33 @@ def tile_liquidmemorycell_pa_k_kernel(
     nc = tc.nc
 
     units = []
-    first_group = 0
-    for n_groups in CHUNK_GROUPS:
+    runs = []
+    w1_after = {}
+    for c, (g, n_groups) in enumerate(CHUNKS):
         for m in range(M_TILES):
-            for g in range(first_group, first_group + n_groups, UNIT_GROUPS):
-                units.append((g, m))
-        first_group += n_groups
-    assert first_group == N_GROUPS
-    n_units = len(units)
+            i = len(units)
+            if m == 0:
+                w1_after.setdefault(i + (W1_BEHIND if i else 0), []).append((g, n_groups))
+            if c in SINGLE_CHUNKS or m % 2 == 0:
+                runs.append([])
+            runs[-1].append(i)
+            units.append((g, n_groups, m))
+    n_units, n_runs = len(units), len(runs)
     half_way = n_units // 2
+    lag = [1 if units[run[0]][1] == UNIT_GROUPS else 2 for run in runs]
     completes = {}
-    for i in range(n_units):
-        if units[i][0] + UNIT_GROUPS == N_GROUPS:
-            completes[i + LAG] = units[i][1]
+    for r in range(n_runs):
+        for i in runs[r]:
+            g0, n_groups, m = units[i]
+            if g0 == CHUNKS[-1][0]:
+                completes.setdefault(r + lag[r], []).append(m)
 
     with ExitStack() as ctx:
         const = ctx.enter_context(tc.tile_pool(name="const", bufs=1))
         rows_pool = ctx.enter_context(tc.tile_pool(name="rows", bufs=LOOKAHEAD + 1))
         sorted_pool = ctx.enter_context(tc.tile_pool(name="sorted", bufs=SORT_AHEAD + 2))
         grouped_pool = ctx.enter_context(tc.tile_pool(name="grouped", bufs=3))
-        codes_pool = ctx.enter_context(tc.tile_pool(name="codes", bufs=LAG + 2))
+        codes_pool = ctx.enter_context(tc.tile_pool(name="codes", bufs=6))
         tail_pool = ctx.enter_context(tc.tile_pool(name="tail", bufs=2))
         acc_pool = ctx.enter_context(tc.psum_pool(name="acc", bufs=1))
         bank_pool = ctx.enter_context(tc.psum_pool(name="banks", bufs=4))
@@ -90,42 +97,43 @@ def tile_liquidmemorycell_pa_k_kernel(
         result = const.tile([P, M_TILES, MEM], F32)
         acc = [acc_pool.tile([P, FEATURES], F32, name="acc%d" % m) for m in range(M_TILES)]
 
-        rows, pairs_sorted, codes, planes = {}, {}, {}, {}
-        shifted, mean_var, rstd, normed, t_codes, t_plane = {}, {}, {}, {}, {}, {}
+        rows, pairs_sorted, grouped, codes, planes = {}, {}, {}, {}, {}
+        shifted, mean_var, rstd, normed, t_planes, t_codes, t_plane = {}, {}, {}, {}, {}, {}, {}
 
         def load_rows(i):
-            g0, m = units[i]
-            rows[i] = rows_pool.tile([P, UNIT_COLS], BF16, name="rows")
+            g0, n_groups, m = units[i]
+            n_cols = n_groups * K_PASS
+            rows[i] = rows_pool.tile([P, n_cols], BF16, name="rows")
             batch = slice(m * P, (m + 1) * P)
             if g0 == 0:
                 nc.sync.dma_start(out=rows[i][:, 0:MEM], in_=h[batch, :])
-                nc.sync.dma_start(out=rows[i][:, MEM:], in_=x[batch, 0 : UNIT_COLS - MEM])
+                nc.sync.dma_start(out=rows[i][:, MEM:], in_=x[batch, 0 : n_cols - MEM])
             else:
                 first = g0 * K_PASS - MEM
-                nc.sync.dma_start(out=rows[i][:], in_=x[batch, first : first + UNIT_COLS])
+                nc.sync.dma_start(out=rows[i][:], in_=x[batch, first : first + n_cols])
 
-        def load_w1(g0):
-            for quadrant in range(4):
-                nc.sync.dma_start(
-                    out=w1_planes[g0 // PLANE_GROUPS][32 * quadrant : 32 * quadrant + 16, :].bitcast(I32),
-                    in_=W1_scales[g0 : g0 + PLANE_GROUPS, 4 * quadrant : 4 * quadrant + 4, :].bitcast(I32),
-                )
-            some = slice(g0, g0 + UNIT_GROUPS)
+        def load_w1(g0, n_groups):
+            if g0 == CHUNKS[0][0] or g0 >= PLANE_GROUPS:
+                p0 = g0 - g0 % PLANE_GROUPS
+                for quadrant in range(4):
+                    nc.sync.dma_start(
+                        out=w1_planes[p0 // PLANE_GROUPS][32 * quadrant : 32 * quadrant + 16, :].bitcast(I32),
+                        in_=W1_scales[p0 : p0 + PLANE_GROUPS, 4 * quadrant : 4 * quadrant + 4, :].bitcast(I32),
+                    )
+            some = slice(g0, g0 + n_groups)
             nc.sync.dma_start(
                 out=w1_words[:, some, :].bitcast(I32),
                 in_=W1_words[some].rearrange("g p n t -> p g (n t)").bitcast(I32),
             )
 
-        def load_small():
-            nc.sync.dma_start(out=bias_rows[0:1, 0:FEATURES], in_=b1.unsqueeze(0))
-            nc.sync.dma_start(out=bias_rows[0:1, FEATURES:], in_=b2.unsqueeze(0))
-            nc.sync.dma_start(out=g1_bf[:], in_=g1.rearrange("(p t) -> p t", t=PACK))
-            nc.sync.dma_start(out=be1_bf[:], in_=be1.rearrange("(p t) -> p t", t=PACK))
-            nc.sync.dma_start(
-                out=w2_words[:].bitcast(I32),
-                in_=W2_words[0].rearrange("p n t -> p (n t)").bitcast(I32),
-            )
-            for quadrant in range(4):
+        def load_w2(part):
+            if part == 0:
+                nc.sync.dma_start(
+                    out=w2_words[:].bitcast(I32),
+                    in_=W2_words[0].rearrange("p n t -> p (n t)").bitcast(I32),
+                )
+            else:
+                quadrant = part - 1
                 nc.sync.dma_start(
                     out=w2_plane[32 * quadrant : 32 * quadrant + 4, :].bitcast(I32),
                     in_=W2_scales[0, 4 * quadrant : 4 * quadrant + 4, :].bitcast(I32),
@@ -133,22 +141,23 @@ def tile_liquidmemorycell_pa_k_kernel(
 
         def request(i):
             load_rows(i)
-            if i >= LAG and units[i - LAG][1] == 0:
-                load_w1(units[i - LAG][0])
-            if i == half_way:
-                load_small()
+            for g0, n_groups in w1_after.get(i, []):
+                load_w1(g0, n_groups)
+            if 0 <= i - half_way < 5:
+                load_w2(i - half_way)
 
         def sort_pairs(i):
-            pairs_sorted[i] = sorted_pool.tile([P, UNIT_GROUPS, PAIRS, P], F32, name="pairs_sorted")
+            pairs_sorted[i] = sorted_pool.tile([P, units[i][1], PAIRS, P], F32, name="pairs_sorted")
             nc.vector.tensor_copy(
                 out=pairs_sorted[i][:],
                 in_=rows[i][:].bitcast(F32).rearrange("b (g p u) -> b g u p", p=P, u=PAIRS),
             )
 
         def transpose_unit(i):
-            grouped = grouped_pool.tile([P, UNIT_GROUPS * P * PACK], BF16, name="grouped", align_bytes=64)
-            grouped_pairs = grouped[:].bitcast(F32).rearrange("p (g b u) -> p g b u", b=P, u=PAIRS)
-            for g in range(0, UNIT_GROUPS, GROUPS_PER_BANK):
+            n_groups = units[i][1]
+            grouped[i] = grouped_pool.tile([P, n_groups * P * PACK], BF16, name="grouped", align_bytes=64)
+            grouped_pairs = grouped[i][:].bitcast(F32).rearrange("p (g b u) -> p g b u", b=P, u=PAIRS)
+            for g in range(0, n_groups, GROUPS_PER_BANK):
                 bank = bank_pool.tile([P, GROUPS_PER_BANK, PAIRS, P], F32, name="bank")
                 for gg in range(GROUPS_PER_BANK):
                     for u in range(PAIRS):
@@ -159,16 +168,16 @@ def tile_liquidmemorycell_pa_k_kernel(
                     out=grouped_pairs[:, g : g + GROUPS_PER_BANK, :, :],
                     in_=bank[:].rearrange("p g u b -> p g b u"),
                 )
-            return grouped
 
-        def quantise_unit(i, grouped):
-            codes[i] = codes_pool.tile([P, UNIT_GROUPS * P], U32, name="codes", align_bytes=64)
-            planes[i] = codes_pool.tile([P, UNIT_GROUPS * P], U8, name="planes", align_bytes=64)
-            nc.vector.quantize_mx(out=codes[i][:].bitcast(FP8X4), scales=planes[i][:], in_=grouped[:])
+        def quantise_unit(i):
+            n_words = units[i][1] * P
+            codes[i] = codes_pool.tile([P, n_words], U32, name="codes", align_bytes=64)
+            planes[i] = codes_pool.tile([P, n_words], U8, name="planes", align_bytes=64)
+            nc.vector.quantize_mx(out=codes[i][:].bitcast(FP8X4), scales=planes[i][:], in_=grouped[i][:])
 
         def multiply_unit(i):
-            g0, m = units[i]
-            for gi in range(UNIT_GROUPS):
+            g0, n_groups, m = units[i]
+            for gi in range(n_groups):
                 g = g0 + gi
                 cols = slice(gi * P, (gi + 1) * P)
                 nc.tensor.matmul_mx(
@@ -177,7 +186,7 @@ def tile_liquidmemorycell_pa_k_kernel(
                     lhsT_scale=planes[i][:, cols],
                     rhs=w1_words[:, g, :].bitcast(FP8X4),
                     rhs_scale=w1_planes[g // PLANE_GROUPS][PLANE_ROWS * (g % PLANE_GROUPS) :, :],
-                    start=(g == 0),
+                    start=(g == CHUNKS[0][0]),
                     stop=(g == N_GROUPS - 1),
                 )
 
@@ -219,21 +228,23 @@ def tile_liquidmemorycell_pa_k_kernel(
                 op1=ALU.mult,
             )
 
-        def gelu_and_quantise(m):
+        def flip_and_gelu(m):
             flipped = acc_pool.tile([P, PACK, P], F32, name="flipped%d" % m, tag="acc%d" % m)
-            t_planes = tail_pool.tile([P, PACK, P], BF16, name="t_planes")
+            t_planes[m] = tail_pool.tile([P, PACK, P], BF16, name="t_planes")
             for t in range(PACK):
                 nc.tensor.transpose(out=flipped[:, t, :], in_=normed[m][:, t, :], identity=ident[:])
             for t in range(PACK):
                 nc.scalar.activation(
-                    out=t_planes[:, t, :],
+                    out=t_planes[m][:, t, :],
                     in_=flipped[:, t, :],
                     func=ACT.Gelu,
                     bias=be1_col[:, t : t + 1],
                     scale=g1_col[:, t : t + 1],
                 )
+
+        def quantise_t(m):
             t_grouped = tail_pool.tile([P, P, PACK], BF16, name="t_grouped", align_bytes=64)
-            nc.vector.tensor_copy(out=t_grouped[:], in_=t_planes[:].rearrange("p t b -> p b t"))
+            nc.vector.tensor_copy(out=t_grouped[:], in_=t_planes[m][:].rearrange("p t b -> p b t"))
             t_codes[m] = tail_pool.tile([P, P], U32, name="t_codes", align_bytes=64)
             t_plane[m] = tail_pool.tile([P, P], U8, name="t_plane", align_bytes=64)
             nc.vector.quantize_mx(
@@ -264,6 +275,10 @@ def tile_liquidmemorycell_pa_k_kernel(
         make_identity(nc, ident[:])
         nc.gpsimd.memset(bias_rows[:], 0.0)
         nc.gpsimd.memset(ones[:], 1.0)
+        nc.gpsimd.dma_start(out=bias_rows[0:1, 0:FEATURES], in_=b1.unsqueeze(0))
+        nc.gpsimd.dma_start(out=bias_rows[0:1, FEATURES:], in_=b2.unsqueeze(0))
+        nc.gpsimd.dma_start(out=g1_bf[:], in_=g1.rearrange("(p t) -> p t", t=PACK))
+        nc.gpsimd.dma_start(out=be1_bf[:], in_=be1.rearrange("(p t) -> p t", t=PACK))
         nc.gpsimd.memset(neg_half[:], -0.5)
         nc.scalar.activation(out=warm_out[:], in_=warm_in[:], func=ACT.Gelu)
 
@@ -272,22 +287,27 @@ def tile_liquidmemorycell_pa_k_kernel(
         for i in range(SORT_AHEAD):
             sort_pairs(i)
 
-        for i in range(n_units + LAG + SECOND_AT):
-            if i + LOOKAHEAD < n_units:
-                request(i + LOOKAHEAD)
-            if i + SORT_AHEAD < n_units:
-                sort_pairs(i + SORT_AHEAD)
-            if i - GELU_AT in completes:
-                gelu_and_quantise(completes[i - GELU_AT])
-            if i < n_units:
-                quantise_unit(i, transpose_unit(i))
-            if LAG <= i < n_units + LAG:
-                multiply_unit(i - LAG)
-            if i == half_way:
+        for r in range(n_runs + 4):
+            for i in runs[r] if r < n_runs else []:
+                if i + LOOKAHEAD < n_units:
+                    request(i + LOOKAHEAD)
+                if i + SORT_AHEAD < n_units:
+                    sort_pairs(i + SORT_AHEAD)
+                transpose_unit(i)
+                quantise_unit(i)
+            for q in range(n_runs):
+                if q + lag[q] == r:
+                    for i in runs[q]:
+                        multiply_unit(i)
+            if r == n_runs // 2:
                 broadcast_biases()
-            if i - SECOND_AT in completes:
-                second_product(completes[i - SECOND_AT])
-            if i - NORMALISE_AT in completes:
-                normalise(completes[i - NORMALISE_AT])
-            if i in completes:
-                statistics(completes[i])
+            for m in completes.get(r, []):
+                statistics(m)
+            for m in completes.get(r - 1, []):
+                normalise(m)
+            for m in completes.get(r - 2, []):
+                flip_and_gelu(m)
+            for m in completes.get(r - 3, []):
+                second_product(m)
+            for m in completes.get(r - 2, []):
+                quantise_t(m)

@@ -26,7 +26,8 @@ GROUPS_PER_BANK = 2
 UNIT_GROUPS = 4
 CHUNKS = ((2, 2), (0, 2)) + tuple((g, 4) for g in range(4, N_GROUPS, 4))
 RUN_GROUPS = 8
-SINGLE_CHUNKS = (0, 1, 2, len(CHUNKS) - 1)
+HEAD_UNITS = 12
+TAIL_UNITS = 6
 PLANE_GROUPS = 4
 PLANE_ROWS = 4
 LOOKAHEAD = 10
@@ -42,17 +43,19 @@ def tile_liquidmemorycell_pa_k_kernel(
     nc = tc.nc
 
     units = []
+    for g, n_groups in CHUNKS:
+        units.extend((g, n_groups, m) for m in range(M_TILES))
+    late = units.pop(-1 - M_TILES)
+    units.insert(-1, late)
     runs = []
     w1_after = {}
-    for c, (g, n_groups) in enumerate(CHUNKS):
-        for m in range(M_TILES):
-            i = len(units)
-            if m == 0:
-                w1_after.setdefault(i + (W1_BEHIND if i else 0), []).append((g, n_groups))
-            if c in SINGLE_CHUNKS or m % 2 == 0:
-                runs.append([])
-            runs[-1].append(i)
-            units.append((g, n_groups, m))
+    for i, (g, n_groups, m) in enumerate(units):
+        if g not in [units[j][0] for j in range(i)]:
+            w1_after.setdefault(i + (W1_BEHIND if i else 0), []).append((g, n_groups))
+        paired = HEAD_UNITS <= i < len(units) - TAIL_UNITS
+        if not paired or (i - HEAD_UNITS) % 2 == 0:
+            runs.append([])
+        runs[-1].append(i)
     n_units, n_runs = len(units), len(runs)
     half_way = n_units // 2
     lag = [1 if units[run[0]][1] == UNIT_GROUPS else 2 for run in runs]
@@ -60,8 +63,8 @@ def tile_liquidmemorycell_pa_k_kernel(
     for r in range(n_runs):
         for i in runs[r]:
             g0, n_groups, m = units[i]
-            if g0 == CHUNKS[-1][0]:
-                completes.setdefault(r + lag[r], []).append(m)
+            if g0 + n_groups == N_GROUPS:
+                completes[r + lag[r]] = m
 
     with ExitStack() as ctx:
         const = ctx.enter_context(tc.tile_pool(name="const", bufs=1))
@@ -69,7 +72,7 @@ def tile_liquidmemorycell_pa_k_kernel(
         sorted_pool = ctx.enter_context(tc.tile_pool(name="sorted", bufs=SORT_AHEAD + 2))
         grouped_pool = ctx.enter_context(tc.tile_pool(name="grouped", bufs=3))
         codes_pool = ctx.enter_context(tc.tile_pool(name="codes", bufs=6))
-        tail_pool = ctx.enter_context(tc.tile_pool(name="tail", bufs=2))
+        tail_pool = ctx.enter_context(tc.tile_pool(name="tail", bufs=M_TILES))
         acc_pool = ctx.enter_context(tc.psum_pool(name="acc", bufs=1))
         bank_pool = ctx.enter_context(tc.psum_pool(name="banks", bufs=4))
         ctx.enter_context(tc.manual_schedule())
@@ -98,7 +101,7 @@ def tile_liquidmemorycell_pa_k_kernel(
         acc = [acc_pool.tile([P, FEATURES], F32, name="acc%d" % m) for m in range(M_TILES)]
 
         rows, pairs_sorted, grouped, codes, planes = {}, {}, {}, {}, {}
-        shifted, mean_var, rstd, normed, t_planes, t_codes, t_plane = {}, {}, {}, {}, {}, {}, {}
+        shifted, stats, mean_var, rstd, normed, t_planes, t_grouped, t_codes, t_plane, product = [{} for j in range(10)]
 
         def load_rows(i):
             g0, n_groups, m = units[i]
@@ -173,7 +176,15 @@ def tile_liquidmemorycell_pa_k_kernel(
             n_words = units[i][1] * P
             codes[i] = codes_pool.tile([P, n_words], U32, name="codes", align_bytes=64)
             planes[i] = codes_pool.tile([P, n_words], U8, name="planes", align_bytes=64)
-            nc.vector.quantize_mx(out=codes[i][:].bitcast(FP8X4), scales=planes[i][:], in_=grouped[i][:])
+            n_parts = 2 if i == n_units - 1 else 1
+            for part in range(n_parts):
+                words = slice(part * n_words // n_parts, (part + 1) * n_words // n_parts)
+                values = slice(PACK * words.start, PACK * words.stop)
+                nc.vector.quantize_mx(
+                    out=codes[i][:, words].bitcast(FP8X4),
+                    scales=planes[i][:, words],
+                    in_=grouped[i][:, values],
+                )
 
         def multiply_unit(i):
             g0, n_groups, m = units[i]
@@ -200,7 +211,7 @@ def tile_liquidmemorycell_pa_k_kernel(
             nc.gpsimd.tensor_copy(out=g1_col[:], in_=g1_bf[:])
             nc.gpsimd.tensor_copy(out=be1_col[:], in_=be1_bf[:])
 
-        def statistics(m):
+        def add_bias(m):
             shifted[m] = tail_pool.tile([P, PACK, P], F32, name="shifted")
             nc.vector.tensor_tensor(
                 out=shifted[m][:],
@@ -208,10 +219,16 @@ def tile_liquidmemorycell_pa_k_kernel(
                 in1=b1_sorted[:],
                 op=ALU.add,
             )
-            stats = tail_pool.tile([P, 6], F32, name="stats")
-            nc.vector.bn_stats(out=stats[:], in_=shifted[m][:].rearrange("b t p -> b (t p)"))
+
+        def take_stats(m):
+            stats[m] = tail_pool.tile([P, 6], F32, name="stats")
+            nc.vector.bn_stats(out=stats[m][:], in_=shifted[m][:].rearrange("b t p -> b (t p)"))
+
+        def mean_and_var(m):
             mean_var[m] = tail_pool.tile([P, 2], F32, name="mean_var")
-            nc.vector.bn_aggr(out=mean_var[m][:], in_=stats[:])
+            nc.vector.bn_aggr(out=mean_var[m][:], in_=stats[m][:])
+
+        def inverse_std(m):
             var_eps = tail_pool.tile([P, 1], F32, name="var_eps")
             nc.vector.tensor_scalar_add(out=var_eps[:], in0=mean_var[m][:, 1:2], scalar1=LN_EPS)
             rstd[m] = tail_pool.tile([P, 1], F32, name="rstd")
@@ -242,21 +259,23 @@ def tile_liquidmemorycell_pa_k_kernel(
                     scale=g1_col[:, t : t + 1],
                 )
 
+        def group_t(m):
+            t_grouped[m] = tail_pool.tile([P, P, PACK], BF16, name="t_grouped", align_bytes=64)
+            nc.vector.tensor_copy(out=t_grouped[m][:], in_=t_planes[m][:].rearrange("p t b -> p b t"))
+
         def quantise_t(m):
-            t_grouped = tail_pool.tile([P, P, PACK], BF16, name="t_grouped", align_bytes=64)
-            nc.vector.tensor_copy(out=t_grouped[:], in_=t_planes[m][:].rearrange("p t b -> p b t"))
             t_codes[m] = tail_pool.tile([P, P], U32, name="t_codes", align_bytes=64)
             t_plane[m] = tail_pool.tile([P, P], U8, name="t_plane", align_bytes=64)
             nc.vector.quantize_mx(
                 out=t_codes[m][:].bitcast(FP8X4),
                 scales=t_plane[m][:],
-                in_=t_grouped[:].rearrange("p b t -> p (b t)"),
+                in_=t_grouped[m][:].rearrange("p b t -> p (b t)"),
             )
 
         def second_product(m):
-            product = acc_pool.tile([P, MEM], F32, name="product%d" % m, tag="acc%d" % m)
+            product[m] = acc_pool.tile([P, MEM], F32, name="product%d" % m, tag="acc%d" % m)
             nc.tensor.matmul_mx(
-                out=product[:],
+                out=product[m][:],
                 lhsT=t_codes[m][:].bitcast(FP8X4),
                 lhsT_scale=t_plane[m][:],
                 rhs=w2_words[:].bitcast(FP8X4),
@@ -264,7 +283,9 @@ def tile_liquidmemorycell_pa_k_kernel(
                 start=True,
                 stop=True,
             )
-            nc.vector.tensor_tensor(out=pre_tanh[:, m, :], in0=product[:], in1=b2_all[:], op=ALU.add)
+
+        def finish(m):
+            nc.vector.tensor_tensor(out=pre_tanh[:, m, :], in0=product[m][:], in1=b2_all[:], op=ALU.add)
             nc.scalar.activation(out=result[:, m, :], in_=pre_tanh[:, m, :], func=ACT.Tanh)
             nc.sync.dma_start(out=out[m * P : (m + 1) * P, :], in_=result[:, m, :])
 
@@ -287,27 +308,60 @@ def tile_liquidmemorycell_pa_k_kernel(
         for i in range(SORT_AHEAD):
             sort_pairs(i)
 
-        for r in range(n_runs + 4):
-            for i in runs[r] if r < n_runs else []:
-                if i + LOOKAHEAD < n_units:
-                    request(i + LOOKAHEAD)
-                if i + SORT_AHEAD < n_units:
-                    sort_pairs(i + SORT_AHEAD)
-                transpose_unit(i)
+        def prepare(i):
+            if i + LOOKAHEAD < n_units:
+                request(i + LOOKAHEAD)
+            if i + SORT_AHEAD < n_units:
+                sort_pairs(i + SORT_AHEAD)
+            transpose_unit(i)
+
+        for r in range(n_runs):
+            done, before = completes.get(r - 1), completes.get(r - 2)
+            if before is not None:
+                mean_and_var(before)
+            if done is not None:
+                add_bias(done)
+            if before is not None:
+                inverse_std(before)
+            for i in runs[r]:
+                prepare(i)
                 quantise_unit(i)
+            if done is not None:
+                take_stats(done)
+            if before is not None:
+                normalise(before)
             for q in range(n_runs):
                 if q + lag[q] == r:
                     for i in runs[q]:
                         multiply_unit(i)
             if r == n_runs // 2:
                 broadcast_biases()
-            for m in completes.get(r, []):
-                statistics(m)
-            for m in completes.get(r - 1, []):
-                normalise(m)
-            for m in completes.get(r - 2, []):
-                flip_and_gelu(m)
-            for m in completes.get(r - 3, []):
-                second_product(m)
-            for m in completes.get(r - 2, []):
-                quantise_t(m)
+
+        multiply_unit(n_units - 1)
+        mean_and_var(2)
+        inverse_std(2)
+        add_bias(3)
+        normalise(2)
+        for m in range(3):
+            flip_and_gelu(m)
+        take_stats(3)
+        group_t(0)
+        mean_and_var(3)
+        quantise_t(0)
+        inverse_std(3)
+        group_t(1)
+        second_product(0)
+        normalise(3)
+        flip_and_gelu(3)
+        quantise_t(1)
+        group_t(2)
+        second_product(1)
+        finish(0)
+        quantise_t(2)
+        second_product(2)
+        finish(1)
+        finish(2)
+        group_t(3)
+        quantise_t(3)
+        second_product(3)
+        finish(3)

@@ -24,10 +24,15 @@ LN_EPS = 1e-5
 
 GROUPS_PER_BANK = 2
 UNIT_GROUPS = 4
-CHUNKS = ((2, 2), (0, 2)) + tuple((g, 4) for g in range(4, N_GROUPS, 4))
+CHUNKS = (
+    ((2, 2),)
+    + tuple((g, 4) for g in range(4, N_GROUPS - 8, 4))
+    + ((0, 2), (N_GROUPS - 8, 4), (N_GROUPS - 4, 4))
+)
 RUN_GROUPS = 8
 HEAD_UNITS = 12
-TAIL_UNITS = 6
+HEAD_LAG = 8
+TAIL_UNITS = 4
 PLANE_GROUPS = 4
 PLANE_ROWS = 4
 LOOKAHEAD = 10
@@ -51,14 +56,13 @@ def tile_liquidmemorycell_pa_k_kernel(
     w1_after = {}
     for i, (g, n_groups, m) in enumerate(units):
         if g not in [units[j][0] for j in range(i)]:
-            w1_after.setdefault(i + (W1_BEHIND if i else 0), []).append((g, n_groups))
+            w1_after.setdefault(i + (W1_BEHIND if n_groups == UNIT_GROUPS else 0), []).append((g, n_groups))
         paired = HEAD_UNITS <= i < len(units) - TAIL_UNITS
         if not paired or (i - HEAD_UNITS) % 2 == 0:
             runs.append([])
         runs[-1].append(i)
     n_units, n_runs = len(units), len(runs)
-    half_way = n_units // 2
-    lag = [1 if units[run[0]][1] == UNIT_GROUPS else 2 for run in runs]
+    lag = [2 if run[0] < HEAD_LAG else 1 for run in runs]
     completes = {}
     for r in range(n_runs):
         for i in runs[r]:
@@ -115,28 +119,29 @@ def tile_liquidmemorycell_pa_k_kernel(
                 first = g0 * K_PASS - MEM
                 nc.sync.dma_start(out=rows[i][:], in_=x[batch, first : first + n_cols])
 
-        def load_w1(g0, n_groups):
-            if g0 == CHUNKS[0][0] or g0 >= PLANE_GROUPS:
-                p0 = g0 - g0 % PLANE_GROUPS
-                for quadrant in range(4):
-                    nc.sync.dma_start(
-                        out=w1_planes[p0 // PLANE_GROUPS][32 * quadrant : 32 * quadrant + 16, :].bitcast(I32),
-                        in_=W1_scales[p0 : p0 + PLANE_GROUPS, 4 * quadrant : 4 * quadrant + 4, :].bitcast(I32),
-                    )
+        def load_scales(v):
+            four = slice(PLANE_GROUPS * v, PLANE_GROUPS * (v + 1))
+            for quadrant in range(4):
+                nc.sync.dma_start(
+                    out=w1_planes[v][32 * quadrant : 32 * quadrant + 16, :].bitcast(I32),
+                    in_=W1_scales[four, 4 * quadrant : 4 * quadrant + 4, :].bitcast(I32),
+                )
+
+        def load_words(g0, n_groups):
             some = slice(g0, g0 + n_groups)
             nc.sync.dma_start(
                 out=w1_words[:, some, :].bitcast(I32),
                 in_=W1_words[some].rearrange("g p n t -> p g (n t)").bitcast(I32),
             )
 
-        def load_w2(part):
-            if part == 0:
-                nc.sync.dma_start(
-                    out=w2_words[:].bitcast(I32),
-                    in_=W2_words[0].rearrange("p n t -> p (n t)").bitcast(I32),
-                )
-            else:
-                quadrant = part - 1
+        def load_rest():
+            nc.sync.dma_start(out=g1_bf[:], in_=g1.rearrange("(p t) -> p t", t=PACK))
+            nc.sync.dma_start(out=be1_bf[:], in_=be1.rearrange("(p t) -> p t", t=PACK))
+            nc.sync.dma_start(
+                out=w2_words[:].bitcast(I32),
+                in_=W2_words[0].rearrange("p n t -> p (n t)").bitcast(I32),
+            )
+            for quadrant in range(4):
                 nc.sync.dma_start(
                     out=w2_plane[32 * quadrant : 32 * quadrant + 4, :].bitcast(I32),
                     in_=W2_scales[0, 4 * quadrant : 4 * quadrant + 4, :].bitcast(I32),
@@ -145,9 +150,13 @@ def tile_liquidmemorycell_pa_k_kernel(
         def request(i):
             load_rows(i)
             for g0, n_groups in w1_after.get(i, []):
-                load_w1(g0, n_groups)
-            if 0 <= i - half_way < 5:
-                load_w2(i - half_way)
+                if g0 >= PLANE_GROUPS:
+                    load_scales(g0 // PLANE_GROUPS)
+                load_words(g0, n_groups)
+            if i == 1:
+                load_scales(0)
+            if i == n_units - 1:
+                load_rest()
 
         def sort_pairs(i):
             pairs_sorted[i] = sorted_pool.tile([P, units[i][1], PAIRS, P], F32, name="pairs_sorted")
@@ -208,8 +217,6 @@ def tile_liquidmemorycell_pa_k_kernel(
             b2_bank = bank_pool.tile([P, MEM], F32, name="b2_bank", tag="bank")
             nc.tensor.matmul(out=b2_bank[:], lhsT=ones[:], rhs=bias_rows[:, FEATURES:], start=True, stop=True)
             nc.scalar.copy(out=b2_all[:], in_=b2_bank[:])
-            nc.gpsimd.tensor_copy(out=g1_col[:], in_=g1_bf[:])
-            nc.gpsimd.tensor_copy(out=be1_col[:], in_=be1_bf[:])
 
         def add_bias(m):
             shifted[m] = tail_pool.tile([P, PACK, P], F32, name="shifted")
@@ -298,8 +305,6 @@ def tile_liquidmemorycell_pa_k_kernel(
         nc.gpsimd.memset(ones[:], 1.0)
         nc.gpsimd.dma_start(out=bias_rows[0:1, 0:FEATURES], in_=b1.unsqueeze(0))
         nc.gpsimd.dma_start(out=bias_rows[0:1, FEATURES:], in_=b2.unsqueeze(0))
-        nc.gpsimd.dma_start(out=g1_bf[:], in_=g1.rearrange("(p t) -> p t", t=PACK))
-        nc.gpsimd.dma_start(out=be1_bf[:], in_=be1.rearrange("(p t) -> p t", t=PACK))
         nc.gpsimd.memset(neg_half[:], -0.5)
         nc.scalar.activation(out=warm_out[:], in_=warm_in[:], func=ACT.Gelu)
 
@@ -337,18 +342,21 @@ def tile_liquidmemorycell_pa_k_kernel(
             if r == n_runs // 2:
                 broadcast_biases()
 
+        nc.gpsimd.tensor_copy(out=g1_col[:], in_=g1_bf[:])
+        nc.gpsimd.tensor_copy(out=be1_col[:], in_=be1_bf[:])
         multiply_unit(n_units - 1)
         mean_and_var(2)
         inverse_std(2)
         add_bias(3)
-        normalise(2)
-        for m in range(3):
+        for m in range(2):
             flip_and_gelu(m)
         take_stats(3)
-        group_t(0)
         mean_and_var(3)
-        quantise_t(0)
         inverse_std(3)
+        normalise(2)
+        group_t(0)
+        flip_and_gelu(2)
+        quantise_t(0)
         group_t(1)
         second_product(0)
         normalise(3)

@@ -30,14 +30,16 @@ CHUNKS = (
     + ((0, 2), (N_GROUPS - 8, 4), (N_GROUPS - 4, 4))
 )
 RUN_GROUPS = 8
-HEAD_UNITS = 12
-HEAD_LAG = 8
+HEAD_UNITS = 4
+HEAD_LAG = 4
 TAIL_UNITS = 4
 PLANE_GROUPS = 4
 PLANE_ROWS = 4
 LOOKAHEAD = 10
 SORT_AHEAD = 2
-W1_BEHIND = 2
+W1_BEHIND = 3
+
+HALVES = (slice(0, PACK // 2), slice(PACK // 2, PACK))
 
 FLOPS = 2 * BATCH * (MEM + IN_DIM) * FEATURES + 2 * BATCH * FEATURES * MEM
 
@@ -220,47 +222,56 @@ def tile_liquidmemorycell_pa_k_kernel(
 
         def add_bias(m):
             shifted[m] = tail_pool.tile([P, PACK, P], F32, name="shifted")
-            nc.vector.tensor_tensor(
-                out=shifted[m][:],
-                in0=acc[m][:].rearrange("b (p t) -> b t p", t=PACK),
-                in1=b1_sorted[:],
-                op=ALU.add,
-            )
+            for half in HALVES:
+                nc.vector.tensor_tensor(
+                    out=shifted[m][:, half, :],
+                    in0=acc[m][:].rearrange("b (p t) -> b t p", t=PACK)[:, half, :],
+                    in1=b1_sorted[:, half, :],
+                    op=ALU.add,
+                )
 
         def take_stats(m):
-            stats[m] = tail_pool.tile([P, 6], F32, name="stats")
-            nc.vector.bn_stats(out=stats[m][:], in_=shifted[m][:].rearrange("b t p -> b (t p)"))
+            stats[m] = tail_pool.tile([P, 2, 6], F32, name="stats")
+            for j, half in enumerate(HALVES):
+                nc.vector.bn_stats(out=stats[m][:, j, :], in_=shifted[m][:, half, :].rearrange("b t p -> b (t p)"))
+            nc.vector.tensor_scalar_add(
+                out=stats[m][:, 0, 2:3], in0=stats[m][:, 0, 2:3], scalar1=LN_EPS * FEATURES
+            )
 
         def mean_and_var(m):
             mean_var[m] = tail_pool.tile([P, 2], F32, name="mean_var")
-            nc.vector.bn_aggr(out=mean_var[m][:], in_=stats[m][:])
+            nc.vector.bn_aggr(out=mean_var[m][:], in_=stats[m][:].rearrange("b j s -> b (j s)"))
 
         def inverse_std(m):
-            var_eps = tail_pool.tile([P, 1], F32, name="var_eps")
-            nc.vector.tensor_scalar_add(out=var_eps[:], in0=mean_var[m][:, 1:2], scalar1=LN_EPS)
             rstd[m] = tail_pool.tile([P, 1], F32, name="rstd")
-            nc.gpsimd.tensor_tensor(out=rstd[m][:], in0=var_eps[:], in1=neg_half[:], op=ALU.pow)
+            nc.gpsimd.tensor_tensor(out=rstd[m][:], in0=mean_var[m][:, 1:2], in1=neg_half[:], op=ALU.pow)
 
         def normalise(m):
             normed[m] = tail_pool.tile([P, PACK, P], F32, name="normed")
-            nc.vector.tensor_scalar(
-                out=normed[m][:],
-                in0=shifted[m][:],
-                scalar1=mean_var[m][:, 0:1],
-                scalar2=rstd[m][:],
-                op0=ALU.subtract,
-                op1=ALU.mult,
-            )
+            for half in HALVES:
+                nc.vector.tensor_scalar(
+                    out=normed[m][:, half, :],
+                    in0=shifted[m][:, half, :],
+                    scalar1=mean_var[m][:, 0:1],
+                    scalar2=rstd[m][:],
+                    op0=ALU.subtract,
+                    op1=ALU.mult,
+                )
 
         def flip_and_gelu(m):
-            flipped = acc_pool.tile([P, PACK, P], F32, name="flipped%d" % m, tag="acc%d" % m)
+            flipped = (
+                acc_pool.tile([P, PACK // 2, P], F32, name="flipped%d" % m, tag="acc%d" % m),
+                bank_pool.tile([P, PACK // 2, P], F32, name="flipped", tag="bank"),
+            )
             t_planes[m] = tail_pool.tile([P, PACK, P], BF16, name="t_planes")
             for t in range(PACK):
-                nc.tensor.transpose(out=flipped[:, t, :], in_=normed[m][:, t, :], identity=ident[:])
+                nc.tensor.transpose(
+                    out=flipped[t // 2][:, t % 2, :], in_=normed[m][:, t, :], identity=ident[:]
+                )
             for t in range(PACK):
                 nc.scalar.activation(
                     out=t_planes[m][:, t, :],
-                    in_=flipped[:, t, :],
+                    in_=flipped[t // 2][:, t % 2, :],
                     func=ACT.Gelu,
                     bias=be1_col[:, t : t + 1],
                     scale=g1_col[:, t : t + 1],
@@ -268,16 +279,20 @@ def tile_liquidmemorycell_pa_k_kernel(
 
         def group_t(m):
             t_grouped[m] = tail_pool.tile([P, P, PACK], BF16, name="t_grouped", align_bytes=64)
-            nc.vector.tensor_copy(out=t_grouped[m][:], in_=t_planes[m][:].rearrange("p t b -> p b t"))
+            for half in (slice(0, P // 2), slice(P // 2, P)):
+                nc.vector.tensor_copy(
+                    out=t_grouped[m][:, half, :], in_=t_planes[m][:, :, half].rearrange("p t b -> p b t")
+                )
 
         def quantise_t(m):
             t_codes[m] = tail_pool.tile([P, P], U32, name="t_codes", align_bytes=64)
             t_plane[m] = tail_pool.tile([P, P], U8, name="t_plane", align_bytes=64)
-            nc.vector.quantize_mx(
-                out=t_codes[m][:].bitcast(FP8X4),
-                scales=t_plane[m][:],
-                in_=t_grouped[m][:].rearrange("p b t -> p (b t)"),
-            )
+            for half in (slice(0, P // 2), slice(P // 2, P)):
+                nc.vector.quantize_mx(
+                    out=t_codes[m][:, half].bitcast(FP8X4),
+                    scales=t_plane[m][:, half],
+                    in_=t_grouped[m][:, half, :].rearrange("p b t -> p (b t)"),
+                )
 
         def second_product(m):
             product[m] = acc_pool.tile([P, MEM], F32, name="product%d" % m, tag="acc%d" % m)
@@ -292,8 +307,11 @@ def tile_liquidmemorycell_pa_k_kernel(
             )
 
         def finish(m):
-            nc.vector.tensor_tensor(out=pre_tanh[:, m, :], in0=product[m][:], in1=b2_all[:], op=ALU.add)
-            nc.scalar.activation(out=result[:, m, :], in_=pre_tanh[:, m, :], func=ACT.Tanh)
+            for half in (slice(0, MEM // 2), slice(MEM // 2, MEM)):
+                nc.vector.tensor_tensor(
+                    out=pre_tanh[:, m, half], in0=product[m][:, half], in1=b2_all[:, half], op=ALU.add
+                )
+                nc.scalar.activation(out=result[:, m, half], in_=pre_tanh[:, m, half], func=ACT.Tanh)
             nc.sync.dma_start(out=out[m * P : (m + 1) * P, :], in_=result[:, m, :])
 
         for plane_tile in w1_planes:
@@ -339,7 +357,7 @@ def tile_liquidmemorycell_pa_k_kernel(
                 if q + lag[q] == r:
                     for i in runs[q]:
                         multiply_unit(i)
-            if r == n_runs // 2:
+            if r == HEAD_UNITS:
                 broadcast_biases()
 
         nc.gpsimd.tensor_copy(out=g1_col[:], in_=g1_bf[:])

@@ -35,7 +35,8 @@ HEAD_LAG = 4
 TAIL_UNITS = 4
 PLANE_GROUPS = 4
 PLANE_ROWS = 4
-LOOKAHEAD = 10
+LOOKAHEAD = 8
+PAIRED_CHUNKS = tuple(range(16, N_GROUPS - 8, 4))
 SORT_AHEAD = 2
 W1_BEHIND = 3
 
@@ -54,12 +55,20 @@ def tile_liquidmemorycell_pa_k_kernel(
         units.extend((g, n_groups, m) for m in range(M_TILES))
     late = units.pop(-1 - M_TILES)
     units.insert(-1, late)
+    loads = []
+    for i, (g, n_groups, m) in enumerate(units):
+        if not (g in PAIRED_CHUNKS and m % 2):
+            loads.append([])
+        loads[-1].append(i)
+    load_of = {i: n for n, load in enumerate(loads) for i in load}
+    n_loads = len(loads)
     runs = []
     w1_after = {}
     for i, (g, n_groups, m) in enumerate(units):
         if g not in [units[j][0] for j in range(i)]:
-            w1_after.setdefault(i + (W1_BEHIND if n_groups == UNIT_GROUPS else 0), []).append((g, n_groups))
-        paired = HEAD_UNITS <= i < len(units) - TAIL_UNITS
+            behind = 2 if g >= N_GROUPS - 2 * UNIT_GROUPS else W1_BEHIND if n_groups == UNIT_GROUPS else 0
+            w1_after.setdefault(load_of[i + behind], []).append((g, n_groups))
+        paired = HEAD_UNITS <= i < len(units) - TAIL_UNITS or i >= len(units) - 2
         if not paired or (i - HEAD_UNITS) % 2 == 0:
             runs.append([])
         runs[-1].append(i)
@@ -109,17 +118,21 @@ def tile_liquidmemorycell_pa_k_kernel(
         rows, pairs_sorted, grouped, codes, planes = {}, {}, {}, {}, {}
         shifted, stats, mean_var, rstd, normed, t_planes, t_grouped, t_codes, t_plane, product = [{} for j in range(10)]
 
-        def load_rows(i):
-            g0, n_groups, m = units[i]
+        def load_rows(n):
+            g0, n_groups, m = units[loads[n][0]]
             n_cols = n_groups * K_PASS
-            rows[i] = rows_pool.tile([P, n_cols], BF16, name="rows")
-            batch = slice(m * P, (m + 1) * P)
-            if g0 == 0:
-                nc.sync.dma_start(out=rows[i][:, 0:MEM], in_=h[batch, :])
-                nc.sync.dma_start(out=rows[i][:, MEM:], in_=x[batch, 0 : n_cols - MEM])
-            else:
-                first = g0 * K_PASS - MEM
-                nc.sync.dma_start(out=rows[i][:], in_=x[batch, first : first + n_cols])
+            tiles = rows_pool.tile([P, len(loads[n]), n_cols], BF16, name="rows")
+            for place, i in enumerate(loads[n]):
+                rows[i] = tiles[:, place, :]
+            batch = slice(m * P, (m + len(loads[n])) * P)
+            from_h = MEM if g0 == 0 else 0
+            if from_h:
+                nc.sync.dma_start(out=tiles[:, :, 0:from_h], in_=h[batch, :].rearrange("(m p) k -> p m k", p=P))
+            first = g0 * K_PASS - MEM + from_h
+            nc.sync.dma_start(
+                out=tiles[:, :, from_h:],
+                in_=x[batch, first : first + n_cols - from_h].rearrange("(m p) k -> p m k", p=P),
+            )
 
         def load_scales(v):
             four = slice(PLANE_GROUPS * v, PLANE_GROUPS * (v + 1))
@@ -149,22 +162,22 @@ def tile_liquidmemorycell_pa_k_kernel(
                     in_=W2_scales[0, 4 * quadrant : 4 * quadrant + 4, :].bitcast(I32),
                 )
 
-        def request(i):
-            load_rows(i)
-            for g0, n_groups in w1_after.get(i, []):
+        def request(n):
+            load_rows(n)
+            for g0, n_groups in w1_after.get(n, []):
                 if g0 >= PLANE_GROUPS:
                     load_scales(g0 // PLANE_GROUPS)
                 load_words(g0, n_groups)
-            if i == 1:
+            if n == 1:
                 load_scales(0)
-            if i == n_units - 1:
+            if n == n_loads - 1:
                 load_rest()
 
         def sort_pairs(i):
             pairs_sorted[i] = sorted_pool.tile([P, units[i][1], PAIRS, P], F32, name="pairs_sorted")
             nc.vector.tensor_copy(
                 out=pairs_sorted[i][:],
-                in_=rows[i][:].bitcast(F32).rearrange("b (g p u) -> b g u p", p=P, u=PAIRS),
+                in_=rows[i].bitcast(F32).rearrange("b (g p u) -> b g u p", p=P, u=PAIRS),
             )
 
         def transpose_unit(i):
@@ -332,8 +345,9 @@ def tile_liquidmemorycell_pa_k_kernel(
             sort_pairs(i)
 
         def prepare(i):
-            if i + LOOKAHEAD < n_units:
-                request(i + LOOKAHEAD)
+            n = load_of[i]
+            if i == loads[n][0] and n + LOOKAHEAD < n_loads:
+                request(n + LOOKAHEAD)
             if i + SORT_AHEAD < n_units:
                 sort_pairs(i + SORT_AHEAD)
             transpose_unit(i)
@@ -362,7 +376,13 @@ def tile_liquidmemorycell_pa_k_kernel(
 
         nc.gpsimd.tensor_copy(out=g1_col[:], in_=g1_bf[:])
         nc.gpsimd.tensor_copy(out=be1_col[:], in_=be1_bf[:])
-        multiply_unit(n_units - 1)
+        for i in runs[-1]:
+            multiply_unit(i)
+        mean_and_var(1)
+        inverse_std(1)
+        add_bias(2)
+        take_stats(2)
+        normalise(1)
         mean_and_var(2)
         inverse_std(2)
         add_bias(3)

from contextlib import ExitStack

import concourse.mybir as mybir
from concourse.masks import make_identity

F32 = mybir.dt.float32
BF16 = mybir.dt.bfloat16
I32 = mybir.dt.int32
U32 = mybir.dt.uint32
U8 = mybir.dt.uint8
FP8X4 = mybir.dt.float8_e4m3fn_x4
ALU = mybir.AluOpType
ACT = mybir.ActivationFunctionType

P = 128
PACK = 4
PAIRS = 2
K_PASS = P * PACK
BATCH, IN_DIM, MEM = 512, 16128, 256
FEATURES = 2 * MEM
N_GROUPS = (MEM + IN_DIM) // K_PASS
M_TILES = BATCH // P
LN_EPS = 1e-5

GROUPS_PER_BANK = 2
UNIT_GROUPS = 4
CHUNKS = (
    ((2, 2),)
    + tuple((g, 4) for g in range(4, N_GROUPS - 8, 4))
    + ((0, 2), (N_GROUPS - 8, 4), (N_GROUPS - 4, 4))
)
RUN_GROUPS = 8
HEAD_UNITS = 4
HEAD_LAG = 4
TAIL_UNITS = 4
PLANE_GROUPS = 4
PLANE_ROWS = 4
LOOKAHEAD = 8
PAIRED_CHUNKS = tuple(range(16, N_GROUPS - 8, 4))
SORT_AHEAD = 2
W1_BEHIND = 3

HALVES = (slice(0, PACK // 2), slice(PACK // 2, PACK))

FLOPS = 2 * BATCH * (MEM + IN_DIM) * FEATURES + 2 * BATCH * FEATURES * MEM


def tile_liquidmemorycell_pa_k_kernel(
    tc, x, h, W1_words, W1_scales, b1, g1, be1, W2_words, W2_scales, b2, out
):
    nc = tc.nc

    units = []
    for g, n_groups in CHUNKS:
        units.extend((g, n_groups, m) for m in range(M_TILES))
    late = units.pop(-1 - M_TILES)
    units.insert(-1, late)
    loads = []
    for i, (g, n_groups, m) in enumerate(units):
        if not (g in PAIRED_CHUNKS and m % 2):
            loads.append([])
        loads[-1].append(i)
    load_of = {i: n for n, load in enumerate(loads) for i in load}
    n_loads = len(loads)
    runs = []
    w1_after = {}
    for i, (g, n_groups, m) in enumerate(units):
        if g not in [units[j][0] for j in range(i)]:
            behind = 2 if g >= N_GROUPS - 2 * UNIT_GROUPS else W1_BEHIND if n_groups == UNIT_GROUPS else 0
            w1_after.setdefault(load_of[i + behind], []).append((g, n_groups))
        paired = HEAD_UNITS <= i < len(units) - TAIL_UNITS or i >= len(units) - 2
        if not paired or (i - HEAD_UNITS) % 2 == 0:
            runs.append([])
        runs[-1].append(i)
    n_units, n_runs = len(units), len(runs)
    lag = [2 if run[0] < HEAD_LAG else 1 for run in runs]
    completes = {}
    for r in range(n_runs):
        for i in runs[r]:
            g0, n_groups, m = units[i]
            if g0 + n_groups == N_GROUPS:
                completes[r + lag[r]] = m

    with ExitStack() as ctx:
        const = ctx.enter_context(tc.tile_pool(name="const", bufs=1))
        rows_pool = ctx.enter_context(tc.tile_pool(name="rows", bufs=LOOKAHEAD + 1))
        sorted_pool = ctx.enter_context(tc.tile_pool(name="sorted", bufs=SORT_AHEAD + 2))
        grouped_pool = ctx.enter_context(tc.tile_pool(name="grouped", bufs=3))
        codes_pool = ctx.enter_context(tc.tile_pool(name="codes", bufs=6))
        tail_pool = ctx.enter_context(tc.tile_pool(name="tail", bufs=M_TILES))
        acc_pool = ctx.enter_context(tc.psum_pool(name="acc", bufs=1))
        bank_pool = ctx.enter_context(tc.psum_pool(name="banks", bufs=4))
        ctx.enter_context(tc.manual_schedule())

        w1_words = const.tile([P, N_GROUPS, FEATURES], U32, align_bytes=64)
        w1_planes = [
            const.tile([P, FEATURES], U8, name="w1_planes%d" % j, align_bytes=64)
            for j in range(N_GROUPS // PLANE_GROUPS)
        ]
        w2_words = const.tile([P, MEM], U32, align_bytes=64)
        w2_plane = const.tile([P, MEM], U8, align_bytes=64)
        ident = const.tile([P, P], F32)
        ones = const.tile([P, P], BF16)
        bias_rows = const.tile([P, FEATURES + MEM], BF16)
        b1_sorted = const.tile([P, PACK, P], F32)
        b2_all = const.tile([P, MEM], F32)
        g1_bf = const.tile([P, PACK], BF16)
        be1_bf = const.tile([P, PACK], BF16)
        g1_col = const.tile([P, PACK], F32)
        be1_col = const.tile([P, PACK], F32)
        neg_half = const.tile([P, 1], F32)
        warm_in = const.tile([P, 1], F32)
        warm_out = const.tile([P, 1], F32)
        pre_tanh = const.tile([P, M_TILES, MEM], F32)
        result = const.tile([P, M_TILES, MEM], F32)
        acc = [acc_pool.tile([P, FEATURES], F32, name="acc%d" % m) for m in range(M_TILES)]

        rows, pairs_sorted, grouped, codes, planes = {}, {}, {}, {}, {}
        shifted, stats, mean_var, rstd, normed, t_planes, t_grouped, t_codes, t_plane, product = [{} for j in range(10)]

        def load_rows(n):
            g0, n_groups, m = units[loads[n][0]]
            n_cols = n_groups * K_PASS
            tiles = rows_pool.tile([P, len(loads[n]), n_cols], BF16, name="rows")
            for place, i in enumerate(loads[n]):
                rows[i] = tiles[:, place, :]
            batch = slice(m * P, (m + len(loads[n])) * P)
            from_h = MEM if g0 == 0 else 0
            if from_h:
                nc.sync.dma_start(out=tiles[:, :, 0:from_h], in_=h[batch, :].rearrange("(m p) k -> p m k", p=P))
            first = g0 * K_PASS - MEM + from_h
            nc.sync.dma_start(
                out=tiles[:, :, from_h:],
                in_=x[batch, first : first + n_cols - from_h].rearrange("(m p) k -> p m k", p=P),
            )

        def load_scales(v):
            four = slice(PLANE_GROUPS * v, PLANE_GROUPS * (v + 1))
            for quadrant in range(4):
                nc.sync.dma_start(
                    out=w1_planes[v][32 * quadrant : 32 * quadrant + 16, :].bitcast(I32),
                    in_=W1_scales[four, 4 * quadrant : 4 * quadrant + 4, :].bitcast(I32),
                )

        def load_words(g0, n_groups):
            some = slice(g0, g0 + n_groups)
            nc.sync.dma_start(
                out=w1_words[:, some, :].bitcast(I32),
                in_=W1_words[some].rearrange("g p n t -> p g (n t)").bitcast(I32),
            )

        def load_rest():
            nc.sync.dma_start(out=g1_bf[:], in_=g1.rearrange("(p t) -> p t", t=PACK))
            nc.sync.dma_start(out=be1_bf[:], in_=be1.rearrange("(p t) -> p t", t=PACK))
            nc.sync.dma_start(
                out=w2_words[:].bitcast(I32),
                in_=W2_words[0].rearrange("p n t -> p (n t)").bitcast(I32),
            )
            for quadrant in range(4):
                nc.sync.dma_start(
                    out=w2_plane[32 * quadrant : 32 * quadrant + 4, :].bitcast(I32),
                    in_=W2_scales[0, 4 * quadrant : 4 * quadrant + 4, :].bitcast(I32),
                )

        def request(n):
            load_rows(n)
            for g0, n_groups in w1_after.get(n, []):
                if g0 >= PLANE_GROUPS:
                    load_scales(g0 // PLANE_GROUPS)
                load_words(g0, n_groups)
            if n == 1:
                load_scales(0)
            if n == n_loads - 1:
                load_rest()

        def sort_pairs(i):
            pairs_sorted[i] = sorted_pool.tile([P, units[i][1], PAIRS, P], F32, name="pairs_sorted")
            nc.vector.tensor_copy(
                out=pairs_sorted[i][:],
                in_=rows[i].bitcast(F32).rearrange("b (g p u) -> b g u p", p=P, u=PAIRS),
            )

        def transpose_unit(i):
            n_groups = units[i][1]
            grouped[i] = grouped_pool.tile([P, n_groups * P * PACK], BF16, name="grouped", align_bytes=64)
            grouped_pairs = grouped[i][:].bitcast(F32).rearrange("p (g b u) -> p g b u", b=P, u=PAIRS)
            for g in range(0, n_groups, GROUPS_PER_BANK):
                bank = bank_pool.tile([P, GROUPS_PER_BANK, PAIRS, P], F32, name="bank")
                for gg in range(GROUPS_PER_BANK):
                    for u in range(PAIRS):
                        nc.tensor.transpose(
                            out=bank[:, gg, u, :], in_=pairs_sorted[i][:, g + gg, u, :], identity=ident[:]
                        )
                nc.scalar.copy(
                    out=grouped_pairs[:, g : g + GROUPS_PER_BANK, :, :],
                    in_=bank[:].rearrange("p g u b -> p g b u"),
                )

        def quantise_unit(i):
            n_words = units[i][1] * P
            codes[i] = codes_pool.tile([P, n_words], U32, name="codes", align_bytes=64)
            planes[i] = codes_pool.tile([P, n_words], U8, name="planes", align_bytes=64)
            n_parts = 2 if i == n_units - 1 else 1
            for part in range(n_parts):
                words = slice(part * n_words // n_parts, (part + 1) * n_words // n_parts)
                values = slice(PACK * words.start, PACK * words.stop)
                nc.vector.quantize_mx(
                    out=codes[i][:, words].bitcast(FP8X4),
                    scales=planes[i][:, words],
                    in_=grouped[i][:, values],
                )

        def multiply_unit(i):
            g0, n_groups, m = units[i]
            for gi in range(n_groups):
                g = g0 + gi
                cols = slice(gi * P, (gi + 1) * P)
                nc.tensor.matmul_mx(
                    out=acc[m][:],
                    lhsT=codes[i][:, cols].bitcast(FP8X4),
                    lhsT_scale=planes[i][:, cols],
                    rhs=w1_words[:, g, :].bitcast(FP8X4),
                    rhs_scale=w1_planes[g // PLANE_GROUPS][PLANE_ROWS * (g % PLANE_GROUPS) :, :],
                    start=(g == CHUNKS[0][0]),
                    stop=(g == N_GROUPS - 1),
                )

        def broadcast_biases():
            b1_bank = bank_pool.tile([P, FEATURES], F32, name="b1_bank", tag="bank")
            nc.tensor.matmul(out=b1_bank[:], lhsT=ones[:], rhs=bias_rows[:, 0:FEATURES], start=True, stop=True)
            nc.scalar.copy(out=b1_sorted[:], in_=b1_bank[:].rearrange("b (p t) -> b t p", t=PACK))
            b2_bank = bank_pool.tile([P, MEM], F32, name="b2_bank", tag="bank")
            nc.tensor.matmul(out=b2_bank[:], lhsT=ones[:], rhs=bias_rows[:, FEATURES:], start=True, stop=True)
            nc.scalar.copy(out=b2_all[:], in_=b2_bank[:])

        def add_bias(m):
            shifted[m] = tail_pool.tile([P, PACK, P], F32, name="shifted")
            for half in HALVES:
                nc.vector.tensor_tensor(
                    out=shifted[m][:, half, :],
                    in0=acc[m][:].rearrange("b (p t) -> b t p", t=PACK)[:, half, :],
                    in1=b1_sorted[:, half, :],
                    op=ALU.add,
                )

        def take_stats(m):
            stats[m] = tail_pool.tile([P, 2, 6], F32, name="stats")
            for j, half in enumerate(HALVES):
                nc.vector.bn_stats(out=stats[m][:, j, :], in_=shifted[m][:, half, :].rearrange("b t p -> b (t p)"))
            nc.vector.tensor_scalar_add(
                out=stats[m][:, 0, 2:3], in0=stats[m][:, 0, 2:3], scalar1=LN_EPS * FEATURES
            )

        def mean_and_var(m):
            mean_var[m] = tail_pool.tile([P, 2], F32, name="mean_var")
            nc.vector.bn_aggr(out=mean_var[m][:], in_=stats[m][:].rearrange("b j s -> b (j s)"))

        def inverse_std(m):
            rstd[m] = tail_pool.tile([P, 1], F32, name="rstd")
            nc.gpsimd.tensor_tensor(out=rstd[m][:], in0=mean_var[m][:, 1:2], in1=neg_half[:], op=ALU.pow)

        def normalise(m):
            normed[m] = tail_pool.tile([P, PACK, P], F32, name="normed")
            for half in HALVES:
                nc.vector.tensor_scalar(
                    out=normed[m][:, half, :],
                    in0=shifted[m][:, half, :],
                    scalar1=mean_var[m][:, 0:1],
                    scalar2=rstd[m][:],
                    op0=ALU.subtract,
                    op1=ALU.mult,
                )

        def flip_and_gelu(m):
            flipped = (
                acc_pool.tile([P, PACK // 2, P], F32, name="flipped%d" % m, tag="acc%d" % m),
                bank_pool.tile([P, PACK // 2, P], F32, name="flipped", tag="bank"),
            )
            t_planes[m] = tail_pool.tile([P, PACK, P], BF16, name="t_planes")
            for t in range(PACK):
                nc.tensor.transpose(
                    out=flipped[t // 2][:, t % 2, :], in_=normed[m][:, t, :], identity=ident[:]
                )
            for t in range(PACK):
                nc.scalar.activation(
                    out=t_planes[m][:, t, :],
                    in_=flipped[t // 2][:, t % 2, :],
                    func=ACT.Gelu,
                    bias=be1_col[:, t : t + 1],
                    scale=g1_col[:, t : t + 1],
                )

        def group_t(m):
            t_grouped[m] = tail_pool.tile([P, P, PACK], BF16, name="t_grouped", align_bytes=64)
            for half in (slice(0, P // 2), slice(P // 2, P)):
                nc.vector.tensor_copy(
                    out=t_grouped[m][:, half, :], in_=t_planes[m][:, :, half].rearrange("p t b -> p b t")
                )

        def quantise_t(m):
            t_codes[m] = tail_pool.tile([P, P], U32, name="t_codes", align_bytes=64)
            t_plane[m] = tail_pool.tile([P, P], U8, name="t_plane", align_bytes=64)
            for half in (slice(0, P // 2), slice(P // 2, P)):
                nc.vector.quantize_mx(
                    out=t_codes[m][:, half].bitcast(FP8X4),
                    scales=t_plane[m][:, half],
                    in_=t_grouped[m][:, half, :].rearrange("p b t -> p (b t)"),
                )

        def second_product(m):
            product[m] = acc_pool.tile([P, MEM], F32, name="product%d" % m, tag="acc%d" % m)
            nc.tensor.matmul_mx(
                out=product[m][:],
                lhsT=t_codes[m][:].bitcast(FP8X4),
                lhsT_scale=t_plane[m][:],
                rhs=w2_words[:].bitcast(FP8X4),
                rhs_scale=w2_plane[:],
                start=True,
                stop=True,
            )

        def finish(m):
            for half in (slice(0, MEM // 2), slice(MEM // 2, MEM)):
                nc.vector.tensor_tensor(
                    out=pre_tanh[:, m, half], in0=product[m][:, half], in1=b2_all[:, half], op=ALU.add
                )
                nc.scalar.activation(out=result[:, m, half], in_=pre_tanh[:, m, half], func=ACT.Tanh)
            nc.sync.dma_start(out=out[m * P : (m + 1) * P, :], in_=result[:, m, :])

        for plane_tile in w1_planes:
            nc.vector.memset(plane_tile[:].bitcast(I32), 0)
        nc.vector.memset(w2_plane[:].bitcast(I32), 0)
        nc.vector.memset(warm_in[:], 0.0)
        make_identity(nc, ident[:])
        nc.gpsimd.memset(bias_rows[:], 0.0)
        nc.gpsimd.memset(ones[:], 1.0)
        nc.gpsimd.dma_start(out=bias_rows[0:1, 0:FEATURES], in_=b1.unsqueeze(0))
        nc.gpsimd.dma_start(out=bias_rows[0:1, FEATURES:], in_=b2.unsqueeze(0))
        nc.gpsimd.memset(neg_half[:], -0.5)
        nc.scalar.activation(out=warm_out[:], in_=warm_in[:], func=ACT.Gelu)

        for i in range(LOOKAHEAD):
            request(i)
        for i in range(SORT_AHEAD):
            sort_pairs(i)

        def prepare(i):
            n = load_of[i]
            if i == loads[n][0] and n + LOOKAHEAD < n_loads:
                request(n + LOOKAHEAD)
            if i + SORT_AHEAD < n_units:
                sort_pairs(i + SORT_AHEAD)
            transpose_unit(i)

        for r in range(n_runs):
            done, before = completes.get(r - 1), completes.get(r - 2)
            if before is not None:
                mean_and_var(before)
            if done is not None:
                add_bias(done)
            if before is not None:
                inverse_std(before)
            for i in runs[r]:
                prepare(i)
                quantise_unit(i)
            if done is not None:
                take_stats(done)
            if before is not None:
                normalise(before)
            for q in range(n_runs):
                if q + lag[q] == r:
                    for i in runs[q]:
                        multiply_unit(i)
            if r == HEAD_UNITS:
                broadcast_biases()

        nc.gpsimd.tensor_copy(out=g1_col[:], in_=g1_bf[:])
        nc.gpsimd.tensor_copy(out=be1_col[:], in_=be1_bf[:])
        for i in runs[-1]:
            multiply_unit(i)
        mean_and_var(1)
        inverse_std(1)
        add_bias(2)
        take_stats(2)
        normalise(1)
        mean_and_var(2)
        inverse_std(2)
        add_bias(3)
        for m in range(2):
            flip_and_gelu(m)
        take_stats(3)
        mean_and_var(3)
        inverse_std(3)
        normalise(2)
        group_t(0)
        flip_and_gelu(2)
        quantise_t(0)
        group_t(1)
        second_product(0)
        normalise(3)
        flip_and_gelu(3)
        quantise_t(1)
        group_t(2)
        second_product(1)
        finish(0)
        quantise_t(2)
        second_product(2)
        finish(1)
        finish(2)
        group_t(3)
        quantise_t(3)
        second_product(3)
        finish(3)
